import numpy as np
import ml_dtypes


def mxq(x, axis, fmt="e4m3"):
    dtype, down = {"e4m3": (ml_dtypes.float8_e4m3fn, 7), "e5m2": (ml_dtypes.float8_e5m2, 14)}[fmt]
    v = np.moveaxis(np.asarray(x, np.float32).astype(ml_dtypes.bfloat16).astype(np.float64), axis, -1)
    blocks = v.reshape(v.shape[:-1] + (-1, 32))
    amax = np.abs(blocks).max(-1, keepdims=True)
    byte = np.maximum(np.where(amax > 0, np.frexp(amax)[1] - 1 + 127, 0) - down, 1)
    scale = np.exp2(byte - 127.0)
    codes = (blocks / scale).astype(np.float32).astype(dtype).astype(np.float64)
    return np.moveaxis((codes * scale).reshape(v.shape), -1, axis)


WIDE = False


def mx_kscale(k):
    if not WIDE:
        return np.ones(k)
    levels = np.array([10, -10, 5, -5, 0])
    a = np.random.permutation(np.resize(levels, k // 512 * 4)).reshape(k // 512, 4)
    idx = np.arange(k)
    return np.exp2(a[idx // 512, idx % 128 // 32])


BF16 = ml_dtypes.bfloat16


def bf(x):
    return np.asarray(x, np.float32).astype(BF16)


def f64(x):
    return np.asarray(x).astype(np.float64)


E2M1 = np.array([0.0, 0.5, 1.0, 1.5, 2.0, 3.0, 4.0, 6.0, -0.0, -0.5, -1.0, -1.5, -2.0, -3.0, -4.0, -6.0])


def pack_weight(w, fmt):
    k, n = w.shape
    w = f64(bf(w)).reshape(k // 32, 32, n)
    amax = np.abs(w).max(1)
    if fmt == "e4m3":
        byte = np.frexp(amax)[1] - 1 + 127 - 7
    else:
        mant, ex = np.frexp(amax / 6.0)
        byte = np.where(mant > 0.5, ex, ex - 1) + 127
    byte = np.clip(np.where(amax > 0, byte, 1), 1, 254)
    scaled = (w * np.exp2(127.0 - byte)[:, None, :]).reshape(k, n).astype(np.float32)
    by_word = np.ascontiguousarray(scaled.reshape(k // 512, 128, 4, n).transpose(0, 1, 3, 2))
    if fmt == "e4m3":
        words = by_word.astype(ml_dtypes.float8_e4m3fn).view(np.uint8)
    else:
        c = by_word.astype(ml_dtypes.float4_e2m1fn).view(np.uint8) & 0xF
        words = c[..., 0::2] | (c[..., 1::2] << 4)
    return np.ascontiguousarray(words), np.ascontiguousarray(byte.astype(np.uint8).reshape(k // 512, 16, n))


def unpack_weight(words, scales, fmt):
    g, p, n, _ = words.shape
    if fmt == "e4m3":
        vals = np.ascontiguousarray(words).view(ml_dtypes.float8_e4m3fn).astype(np.float64)
    else:
        nib = np.empty((g, p, n, 4), np.uint8)
        nib[..., 0::2] = words & 0xF
        nib[..., 1::2] = words >> 4
        vals = E2M1[nib]
    vals = vals * np.repeat(np.exp2(scales.astype(np.float64) - 127.0), 8, axis=1)[..., None]
    return vals.transpose(0, 1, 3, 2).reshape(g * 512, n)

def pack4(w):
    words, scales = pack_weight(w, "e2m1")
    return words.reshape(words.shape[0], 128, -1), scales


def unpack4(words, scales):
    return unpack_weight(words.reshape(words.shape[0], 128, -1, 2), scales, "e2m1")


BATCH, IN_F, OUT_F = 256, 1024, 1024
NUM_BASIS, DEGREE = 8, 3
K = NUM_BASIS + DEGREE
EPS = 1e-5


def _knots():
    return np.linspace(0.0, 1.0, K + 1)


def _compute_basis(x):
    knots = _knots()
    xa = x[..., None]
    basis = ((xa >= knots[:K]) & (xa < knots[1:K + 1])).astype(np.float64)
    for d in range(1, DEGREE + 1):
        m = K - d
        denom1 = knots[d:K] - knots[:m]
        denom2 = knots[d + 1:K + 1] - knots[1:m + 1]
        safe1 = np.where(denom1 != 0, denom1, 1.0)
        safe2 = np.where(denom2 != 0, denom2, 1.0)
        alpha = np.where(denom1 != 0, (xa - knots[:m]) / safe1, 0.0)
        beta = np.where(denom2 != 0, (knots[d + 1:K + 1] - xa) / safe2, 0.0)
        new = alpha * basis[..., :m] + beta * basis[..., 1:m + 1]
        basis = np.concatenate([new, basis[..., m:]], axis=-1)
    return basis


def setup_inputs():
    s = mx_kscale(IN_F)
    bound_cp = float(np.sqrt(6.0 / (IN_F + K)))
    bound_w = float(np.sqrt(6.0 / (IN_F + OUT_F)))
    x = bf(np.random.uniform(0.0, 0.99, (BATCH, IN_F)) * s)
    control_points = bf(np.random.uniform(-bound_cp, bound_cp, (OUT_F, IN_F, K)))
    w = np.random.uniform(-bound_w, bound_w, (OUT_F, IN_F)) / s
    W_words, W_scales = pack4(np.ascontiguousarray(w.T))
    b = bf(np.random.standard_normal(OUT_F) * 0.1)
    gamma = bf(1.0 + np.random.standard_normal(OUT_F) * 0.1)
    beta = bf(np.random.standard_normal(OUT_F) * 0.1)
    return {"x": x,
            "control_points": control_points,
            "W_words": W_words,
            "W_scales": W_scales,
            "b": b,
            "gamma": gamma,
            "beta": beta}


def reference(x, control_points, W_words, W_scales, b, gamma, beta):
    x = f64(x)
    basis = _compute_basis(x)
    bq = mxq(basis.transpose(2, 0, 1), 2, "e4m3")
    cq = mxq(f64(control_points).transpose(2, 1, 0), 1, "e4m3")
    spline_out = (bq @ cq).sum(axis=0)
    out = spline_out + (mxq(x, 1, "e4m3") @ unpack4(W_words, W_scales)) + f64(b)
    mu = np.mean(out, axis=-1, keepdims=True)
    var = np.mean(np.square(out - mu), axis=-1, keepdims=True)
    return f64(gamma) * (out - mu) / np.sqrt(var + EPS) + f64(beta)

@@ -1,0 +1,235 @@
+from contextlib import ExitStack
+
+from concourse import mybir
+from concourse.masks import make_identity
+
+F32 = mybir.dt.float32
+BF16 = mybir.dt.bfloat16
+U8 = mybir.dt.uint8
+U32 = mybir.dt.uint32
+I32 = mybir.dt.int32
+FP8X4 = mybir.dt.float8_e4m3fn_x4
+FP4X4 = mybir.dt.float4_e2m1fn_x4
+ALU = mybir.AluOpType
+ACT = mybir.ActivationFunctionType
+
+P = 128
+B = 256
+IN_F = 1024
+OUT_F = 1024
+NK = 11
+EPS = 1e-5
+FLOPS = 2 * B * OUT_F * (IN_F * NK + IN_F)
+
+NCHUNK = OUT_F // P
+NSLOT = 2 * NK
+WORDS_Q = 128 * NK
+
+
+def tile_bsplinekan_kernel(tc, x, control_points, W_words, W_scales, b, gamma, beta, out):
+    nc = tc.nc
+    with ExitStack() as ctx:
+        const = ctx.enter_context(tc.tile_pool(name="const", bufs=1))
+        rawp = ctx.enter_context(tc.tile_pool(name="rawp", bufs=2))
+        grpp = ctx.enter_context(tc.tile_pool(name="grpp", bufs=4))
+        codp = ctx.enter_context(tc.tile_pool(name="codp", bufs=2))
+        tmpp = ctx.enter_context(tc.tile_pool(name="tmpp", bufs=2))
+        nbp = ctx.enter_context(tc.tile_pool(name="nbp", bufs=3))
+        lnp = ctx.enter_context(tc.tile_pool(name="lnp", bufs=2))
+        pacc = ctx.enter_context(tc.psum_pool(name="pacc", bufs=1))
+        ptr = ctx.enter_context(tc.psum_pool(name="ptr", bufs=4))
+
+        x_sb = const.tile([P, 2, IN_F], BF16)
+        nc.sync.dma_start(out=x_sb[:], in_=x.rearrange("(h p) i -> p h i", p=P))
+
+        cpv = control_points.rearrange("(c p) i k -> c p (i k)", p=P)
+        raws = []
+        for c in range(2):
+            raw = rawp.tile([P, IN_F * NK], BF16, tag="raw", name="raw%d" % c)
+            nc.sync.dma_start(out=raw[:], in_=cpv[c])
+            raws.append(raw)
+
+        ws = const.tile([P, 2, OUT_F], U8, align_bytes=64)
+        nc.vector.memset(ws[:].bitcast(I32), 0)
+        wt = const.tile([P, 2, 2 * OUT_F], U8, align_bytes=64)
+        nc.sync.dma_start(out=wt[:].bitcast(I32), in_=W_words.bitcast(I32).rearrange("g p n -> p g n"))
+        wsv = W_scales.bitcast(I32)
+        for r in range(4):
+            nc.sync.dma_start(
+                out=ws[r:P:32, :, :].bitcast(I32),
+                in_=wsv[:, r:16:4, :].rearrange("g q n -> q g n"),
+            )
+
+        ident = const.tile([P, P], F32)
+        make_identity(nc, ident[:])
+
+        s_pl = const.tile([P, 2, B, 4], F32)
+        xg = const.tile([P, 2, B, 4], BF16, align_bytes=64)
+        for h in range(2):
+            xw = x_sb[:, h, :].bitcast(F32)
+            pxs = ptr.tile([P, 4, P], F32, tag="pt", name="pxs%d" % h)
+            for u in range(4):
+                nc.tensor.transpose(pxs[:, u, :], xw[:, P * u:P * (u + 1)], ident[:])
+            nc.scalar.activation(
+                out=s_pl[:, :, h * P:(h + 1) * P, :],
+                in_=pxs[:].bitcast(BF16).rearrange("p u (b e) -> p e b u", e=2),
+                func=ACT.Copy,
+                scale=11.0,
+            )
+            pxl = ptr.tile([P, 4, P], F32, tag="pt", name="pxl%d" % h)
+            for g in range(2):
+                for u in range(2):
+                    nc.tensor.transpose(pxl[:, 2 * g + u, :], xw[:, 256 * g + u:256 * (g + 1):2], ident[:])
+            nc.vector.tensor_copy(
+                out=xg[:, :, h * P:(h + 1) * P, :].bitcast(F32),
+                in_=pxl[:].rearrange("p (g u) b -> p g b u", u=2),
+            )
+        xcodes = const.tile([P, 2 * B], U32, align_bytes=64)
+        xscales = const.tile([P, 2 * B], U8, align_bytes=64)
+        nc.vector.quantize_mx(
+            out=xcodes[:].bitcast(FP8X4),
+            scales=xscales[:],
+            in_=xg[:].rearrange("p g b t -> p (g b t)"),
+        )
+
+        bcodes = const.tile([P, NK, 2 * B], U32, align_bytes=64)
+        bscales = const.tile([P, NK, 2 * B], U8, align_bytes=64)
+        HC = 4 * B
+
+        def new_plane(k):
+            return nbp.tile([P, 2, HC], BF16, tag="nb", name="nb%d" % k, align_bytes=64)
+
+        def quantise_plane(k, nb):
+            nc.vector.quantize_mx(
+                out=bcodes[:, k, :].bitcast(FP8X4),
+                scales=bscales[:, k, :],
+                in_=nb[:].rearrange("p e c -> p (e c)"),
+            )
+
+        C2 = (2.0 / 3.0) ** 0.5
+        for rho in range(4):
+            mid = float(rho + 4)
+            lo = new_plane(rho)
+            hi = new_plane(rho + 4)
+            for e in range(2):
+                sv = s_pl[:, e, :, :].rearrange("p b u -> p (b u)")
+                w = tmpp.tile([P, HC], F32, tag="w")
+                nc.scalar.activation(out=w[:], in_=sv, func=ACT.Abs, bias=-mid)
+                nc.scalar.activation(out=w[:], in_=w[:], func=ACT.Abs, bias=-2.0)
+                a2 = tmpp.tile([P, HC], F32, tag="a2")
+                nc.scalar.activation(out=a2[:], in_=w[:], func=ACT.Square, bias=-2.0)
+                h2 = tmpp.tile([P, HC], F32, tag="h2")
+                nc.scalar.activation(out=h2[:], in_=w[:], func=ACT.Square, bias=-C2, scale=C2)
+                nc.vector.scalar_tensor_tensor(out=a2[:], in0=w[:], scalar=2.0, in1=a2[:], op0=ALU.subtract, op1=ALU.mult)
+                nc.vector.scalar_tensor_tensor(out=h2[:], in0=w[:], scalar=1.0, in1=h2[:], op0=ALU.subtract, op1=ALU.mult)
+                nc.vector.tensor_scalar(out=a2[:], in0=a2[:], scalar1=0.0, scalar2=1.0 / 6.0, op0=ALU.min, op1=ALU.mult)
+                nc.vector.scalar_tensor_tensor(out=h2[:], in0=h2[:], scalar=0.0, in1=a2[:], op0=ALU.min, op1=ALU.subtract)
+                nc.vector.scalar_tensor_tensor(out=lo[:, e, :], in0=sv, scalar=mid, in1=h2[:], op0=ALU.is_lt, op1=ALU.mult)
+                nc.vector.scalar_tensor_tensor(out=hi[:, e, :], in0=sv, scalar=mid, in1=h2[:], op0=ALU.is_ge, op1=ALU.mult)
+            quantise_plane(rho, lo)
+            quantise_plane(rho + 4, hi)
+
+        n8 = new_plane(8)
+        n9 = new_plane(9)
+        n10 = new_plane(10)
+        for e in range(2):
+            sv = s_pl[:, e, :, :].rearrange("p b u -> p (b u)")
+            w = tmpp.tile([P, HC], F32, tag="w")
+            nc.scalar.activation(out=w[:], in_=sv, func=ACT.Abs, bias=-9.5)
+            a2 = tmpp.tile([P, HC], F32, tag="a2")
+            nc.vector.tensor_scalar(out=a2[:], in0=w[:], scalar1=1.5, scalar2=-1.5, op0=ALU.min, op1=ALU.add)
+            nc.scalar.activation(out=a2[:], in_=a2[:], func=ACT.Square, scale=0.5 ** 0.5)
+            h2 = tmpp.tile([P, HC], F32, tag="h2")
+            nc.vector.tensor_scalar(out=h2[:], in0=w[:], scalar1=0.5, scalar2=-0.5, op0=ALU.min, op1=ALU.add)
+            nc.scalar.activation(out=h2[:], in_=h2[:], func=ACT.Square, scale=1.5 ** 0.5)
+            nc.vector.tensor_tensor(out=n8[:, e, :], in0=a2[:], in1=h2[:], op=ALU.subtract)
+            w = tmpp.tile([P, HC], F32, tag="w")
+            nc.scalar.activation(out=w[:], in_=sv, func=ACT.Abs, bias=-10.0)
+            nc.scalar.activation(out=n9[:, e, :], in_=w[:], func=ACT.Relu, bias=1.0, scale=-1.0)
+            a2 = tmpp.tile([P, HC], F32, tag="a2")
+            nc.vector.tensor_scalar(out=a2[:], in0=sv, scalar1=11.0, scalar2=None, op0=ALU.is_lt)
+            nc.vector.scalar_tensor_tensor(out=n10[:, e, :], in0=sv, scalar=10.0, in1=a2[:], op0=ALU.is_ge, op1=ALU.mult)
+        quantise_plane(8, n8)
+        quantise_plane(9, n9)
+        quantise_plane(10, n10)
+
+        acc = [[pacc.tile([P, 512], F32, tag="acc%d%d" % (h, q), name="acc%d%d" % (h, q)) for q in range(2)] for h in range(2)]
+        bias_bc = const.tile([P, OUT_F], BF16)
+        gamma_bc = const.tile([P, OUT_F], BF16)
+        beta_bc = const.tile([P, OUT_F], BF16)
+        PIECES = [(0, 8), (8, 16), (16, 20), (20, 22)]
+        evac_no = 0
+        for c in range(NCHUNK):
+            if c < 2:
+                raw = raws[c]
+            else:
+                raw = rawp.tile([P, IN_F * NK], BF16, tag="raw", name="raw%d" % c)
+                nc.sync.dma_start(out=raw[:], in_=cpv[c])
+            if c == 3:
+                nc.sync.dma_start(out=bias_bc[:], in_=b.partition_broadcast(P))
+                nc.sync.dma_start(out=gamma_bc[:], in_=gamma.partition_broadcast(P))
+                nc.sync.dma_start(out=beta_bc[:], in_=beta.partition_broadcast(P))
+            raww = raw[:].bitcast(F32)
+            cc = codp.tile([P, NSLOT, P], U32, tag="cc", align_bytes=64)
+            cs = codp.tile([P, NSLOT, P], U8, tag="cs", align_bytes=64)
+            for (f0, f1) in PIECES:
+                grp = grpp.tile([P, f1 - f0, P, 4], BF16, tag="grp", align_bytes=64)
+                for wd in range(f0 // 2, f1 // 2):
+                    pt = ptr.tile([P, 4, P], F32, tag="pt")
+                    for u in range(4):
+                        st = WORDS_Q * u + wd
+                        nc.tensor.transpose(pt[:, u, :], raww[:, st:st + NK * 127 + 1:NK], ident[:])
+                    src = pt[:].bitcast(BF16).rearrange("p u (o e) -> p e o u", e=2)
+                    dst = grp[:, 2 * wd - f0:2 * wd - f0 + 2, :, :]
+                    if evac_no % 2 == 0:
+                        nc.scalar.copy(out=dst, in_=src)
+                    else:
+                        nc.vector.tensor_copy(out=dst, in_=src)
+                    evac_no += 1
+                nc.vector.quantize_mx(
+                    out=cc[:, f0:f1, :].rearrange("p f o -> p (f o)").bitcast(FP8X4),
+                    scales=cs[:, f0:f1, :].rearrange("p f o -> p (f o)"),
+                    in_=grp[:].rearrange("p f o u -> p (f o u)"),
+                )
+            for h in range(2):
+                dst = acc[h][c // 4][:, (c % 4) * P:(c % 4 + 1) * P]
+                for f in range(NSLOT):
+                    par, k = divmod(f, NK)
+                    col = par * B + h * P
+                    nc.tensor.matmul_mx(
+                        out=dst,
+                        lhsT=bcodes[:, k, col:col + P].bitcast(FP8X4),
+                        lhsT_scale=bscales[:, k, col:col + P],
+                        rhs=cc[:, f, :].bitcast(FP8X4),
+                        rhs_scale=cs[:, f, :],
+                        start=(f == 0),
+                        stop=False,
+                    )
+                for g in range(2):
+                    col = g * B + h * P
+                    nc.tensor.matmul_mx(
+                        out=dst,
+                        lhsT=xcodes[:, col:col + P].bitcast(FP8X4),
+                        lhsT_scale=xscales[:, col:col + P],
+                        rhs=wt[:, g, 2 * P * c:2 * P * (c + 1)].bitcast(FP4X4),
+                        rhs_scale=ws[:, g, P * c:P * (c + 1)],
+                        start=False,
+                        stop=(g == 1),
+                    )
+
+        for h in range(2):
+            y = lnp.tile([P, OUT_F], F32, tag="y")
+            stats = lnp.tile([P, 2, 6], F32, tag="stats")
+            for q in range(2):
+                sl = slice(q * 512, (q + 1) * 512)
+                nc.vector.tensor_tensor(out=y[:, sl], in0=acc[h][q][:], in1=bias_bc[:, sl], op=ALU.add)
+                nc.vector.bn_stats(out=stats[:, q, :], in_=y[:, sl])
+            mv = lnp.tile([P, 2], F32, tag="mv")
+            nc.vector.bn_aggr(out=mv[:], in_=stats[:].rearrange("p q s -> p (q s)"))
+            rstd = lnp.tile([P, 1], F32, tag="rstd")
+            nc.scalar.activation(out=rstd[:], in_=mv[:, 1:2], func=ACT.Sqrt, bias=EPS)
+            nc.vector.reciprocal(out=rstd[:], in_=rstd[:])
+            nc.vector.tensor_scalar(out=y[:], in0=y[:], scalar1=mv[:, 0:1], scalar2=rstd[:], op0=ALU.subtract, op1=ALU.mult)
+            nc.vector.tensor_tensor(out=y[:], in0=y[:], in1=gamma_bc[:], op=ALU.mult)
+            nc.vector.tensor_tensor(out=y[:], in0=y[:], in1=beta_bc[:], op=ALU.add)
+            nc.sync.dma_start(out=out[h * P:(h + 1) * P, :], in_=y[:])

@@ -24,6 +24,9 @@ FLOPS = 2 * B * OUT_F * (IN_F * NK + IN_F)
 NCHUNK = OUT_F // P
 NSLOT = 2 * NK
 WORDS_Q = 128 * NK
+HC = 1024
+S_NUM, S_DEN = 15, 22
+TRAIL = 3
 
 
 def tile_bsplinekan_kernel(tc, x, control_points, W_words, W_scales, b, gamma, beta, out):
@@ -32,9 +35,8 @@ def tile_bsplinekan_kernel(tc, x, control_points, W_words, W_scales, b, gamma, b
         const = ctx.enter_context(tc.tile_pool(name="const", bufs=1))
         rawp = ctx.enter_context(tc.tile_pool(name="rawp", bufs=2))
         grpp = ctx.enter_context(tc.tile_pool(name="grpp", bufs=4))
-        codp = ctx.enter_context(tc.tile_pool(name="codp", bufs=2))
-        tmpp = ctx.enter_context(tc.tile_pool(name="tmpp", bufs=2))
-        nbp = ctx.enter_context(tc.tile_pool(name="nbp", bufs=3))
+        tmpp = ctx.enter_context(tc.tile_pool(name="tmpp", bufs=1))
+        nbp = ctx.enter_context(tc.tile_pool(name="nbp", bufs=4))
         lnp = ctx.enter_context(tc.tile_pool(name="lnp", bufs=2))
         pacc = ctx.enter_context(tc.psum_pool(name="pacc", bufs=1))
         ptr = ctx.enter_context(tc.psum_pool(name="ptr", bufs=4))
@@ -63,19 +65,20 @@ def tile_bsplinekan_kernel(tc, x, control_points, W_words, W_scales, b, gamma, b
         ident = const.tile([P, P], F32)
         make_identity(nc, ident[:])
 
-        s_pl = const.tile([P, 2, B, 4], F32)
+        xp = const.tile([P, 2, 2, P, 4], BF16)
         xg = const.tile([P, 2, B, 4], BF16, align_bytes=64)
         for h in range(2):
             xw = x_sb[:, h, :].bitcast(F32)
             pxs = ptr.tile([P, 4, P], F32, tag="pt", name="pxs%d" % h)
             for u in range(4):
                 nc.tensor.transpose(pxs[:, u, :], xw[:, P * u:P * (u + 1)], ident[:])
-            nc.scalar.activation(
-                out=s_pl[:, :, h * P:(h + 1) * P, :],
-                in_=pxs[:].bitcast(BF16).rearrange("p u (b e) -> p e b u", e=2),
-                func=ACT.Copy,
-                scale=11.0,
-            )
+            src = pxs[:].bitcast(BF16).rearrange("p u (b e) -> p e b u", e=2)
+            if h == 0:
+                nc.scalar.copy(out=xp[:, h, :, :, :], in_=src)
+            else:
+                nc.vector.tensor_copy(out=xp[:, h, :, :, :], in_=src)
+        for h in range(2):
+            xw = x_sb[:, h, :].bitcast(F32)
             pxl = ptr.tile([P, 4, P], F32, tag="pt", name="pxl%d" % h)
             for g in range(2):
                 for u in range(2):
@@ -92,144 +95,201 @@ def tile_bsplinekan_kernel(tc, x, control_points, W_words, W_scales, b, gamma, b
             in_=xg[:].rearrange("p g b t -> p (g b t)"),
         )
 
-        bcodes = const.tile([P, NK, 2 * B], U32, align_bytes=64)
-        bscales = const.tile([P, NK, 2 * B], U8, align_bytes=64)
-        HC = 4 * B
+        bcodes = const.tile([P, NK, 2, 2 * P], U32, align_bytes=64)
+        bscales = const.tile([P, NK, 2, 2 * P], U8, align_bytes=64)
 
-        def new_plane(k):
-            return nbp.tile([P, 2, HC], BF16, tag="nb", name="nb%d" % k, align_bytes=64)
+        def new_plane(k, h):
+            return nbp.tile([P, HC], BF16, tag="nb", name="nb%d_%d" % (k, h), align_bytes=64)
 
-        def quantise_plane(k, nb):
-            nc.vector.quantize_mx(
-                out=bcodes[:, k, :].bitcast(FP8X4),
-                scales=bscales[:, k, :],
-                in_=nb[:].rearrange("p e c -> p (e c)"),
-            )
+        def quantise_plane(k, h, nb):
+            nc.vector.quantize_mx(out=bcodes[:, k, h, :].bitcast(FP8X4), scales=bscales[:, k, h, :], in_=nb[:])
 
         C2 = (2.0 / 3.0) ** 0.5
-        for rho in range(4):
-            mid = float(rho + 4)
-            lo = new_plane(rho)
-            hi = new_plane(rho + 4)
-            for e in range(2):
-                sv = s_pl[:, e, :, :].rearrange("p b u -> p (b u)")
-                w = tmpp.tile([P, HC], F32, tag="w")
-                nc.scalar.activation(out=w[:], in_=sv, func=ACT.Abs, bias=-mid)
-                nc.scalar.activation(out=w[:], in_=w[:], func=ACT.Abs, bias=-2.0)
-                a2 = tmpp.tile([P, HC], F32, tag="a2")
-                nc.scalar.activation(out=a2[:], in_=w[:], func=ACT.Square, bias=-2.0)
-                h2 = tmpp.tile([P, HC], F32, tag="h2")
-                nc.scalar.activation(out=h2[:], in_=w[:], func=ACT.Square, bias=-C2, scale=C2)
-                nc.vector.scalar_tensor_tensor(out=a2[:], in0=w[:], scalar=2.0, in1=a2[:], op0=ALU.subtract, op1=ALU.mult)
-                nc.vector.scalar_tensor_tensor(out=h2[:], in0=w[:], scalar=1.0, in1=h2[:], op0=ALU.subtract, op1=ALU.mult)
-                nc.vector.tensor_scalar(out=a2[:], in0=a2[:], scalar1=0.0, scalar2=1.0 / 6.0, op0=ALU.min, op1=ALU.mult)
-                nc.vector.scalar_tensor_tensor(out=h2[:], in0=h2[:], scalar=0.0, in1=a2[:], op0=ALU.min, op1=ALU.subtract)
-                nc.vector.scalar_tensor_tensor(out=lo[:, e, :], in0=sv, scalar=mid, in1=h2[:], op0=ALU.is_lt, op1=ALU.mult)
-                nc.vector.scalar_tensor_tensor(out=hi[:, e, :], in0=sv, scalar=mid, in1=h2[:], op0=ALU.is_ge, op1=ALU.mult)
-            quantise_plane(rho, lo)
-            quantise_plane(rho + 4, hi)
 
-        n8 = new_plane(8)
-        n9 = new_plane(9)
-        n10 = new_plane(10)
-        for e in range(2):
-            sv = s_pl[:, e, :, :].rearrange("p b u -> p (b u)")
-            w = tmpp.tile([P, HC], F32, tag="w")
-            nc.scalar.activation(out=w[:], in_=sv, func=ACT.Abs, bias=-9.5)
-            a2 = tmpp.tile([P, HC], F32, tag="a2")
+        def cubic_unit(rho, h):
+            mid = float(rho + 4)
+            xv = xp[:, h, :, :, :].rearrange("p e b u -> p (e b u)")
+            lo = new_plane(rho, h)
+            hi = new_plane(rho + 4, h)
+            w = tmpp.tile([P, HC], F32, tag="w", name="w")
+            nc.scalar.activation(out=w[:], in_=xv, func=ACT.Abs, bias=-mid, scale=11.0)
+            nc.scalar.activation(out=w[:], in_=w[:], func=ACT.Abs, bias=-2.0)
+            a2 = tmpp.tile([P, HC], F32, tag="a2", name="a2")
+            nc.scalar.activation(out=a2[:], in_=w[:], func=ACT.Square, bias=-2.0)
+            h2 = tmpp.tile([P, HC], F32, tag="h2", name="h2")
+            nc.scalar.activation(out=h2[:], in_=w[:], func=ACT.Square, bias=-C2, scale=C2)
+            nc.vector.scalar_tensor_tensor(out=a2[:], in0=w[:], scalar=2.0, in1=a2[:], op0=ALU.subtract, op1=ALU.mult)
+            nc.vector.scalar_tensor_tensor(out=h2[:], in0=w[:], scalar=1.0, in1=h2[:], op0=ALU.subtract, op1=ALU.mult)
+            nc.vector.tensor_scalar(out=a2[:], in0=a2[:], scalar1=0.0, scalar2=1.0 / 6.0, op0=ALU.min, op1=ALU.mult)
+            fb = tmpp.tile([P, HC], BF16, tag="fb", name="fb")
+            nc.vector.scalar_tensor_tensor(out=fb[:], in0=h2[:], scalar=0.0, in1=a2[:], op0=ALU.min, op1=ALU.subtract)
+            nc.vector.scalar_tensor_tensor(out=lo[:], in0=xv, scalar=mid / 11.0, in1=fb[:], op0=ALU.is_lt, op1=ALU.mult)
+            nc.vector.tensor_tensor(out=hi[:], in0=fb[:], in1=lo[:], op=ALU.subtract)
+            quantise_plane(rho, h, lo)
+            quantise_plane(rho + 4, h, hi)
+
+        def low_unit_a(h):
+            xv = xp[:, h, :, :, :].rearrange("p e b u -> p (e b u)")
+            n8 = new_plane(8, h)
+            w = tmpp.tile([P, HC], F32, tag="w", name="w")
+            nc.scalar.activation(out=w[:], in_=xv, func=ACT.Abs, bias=-9.5, scale=11.0)
+            a2 = tmpp.tile([P, HC], F32, tag="a2", name="a2")
             nc.vector.tensor_scalar(out=a2[:], in0=w[:], scalar1=1.5, scalar2=-1.5, op0=ALU.min, op1=ALU.add)
             nc.scalar.activation(out=a2[:], in_=a2[:], func=ACT.Square, scale=0.5 ** 0.5)
-            h2 = tmpp.tile([P, HC], F32, tag="h2")
+            h2 = tmpp.tile([P, HC], F32, tag="h2", name="h2")
             nc.vector.tensor_scalar(out=h2[:], in0=w[:], scalar1=0.5, scalar2=-0.5, op0=ALU.min, op1=ALU.add)
             nc.scalar.activation(out=h2[:], in_=h2[:], func=ACT.Square, scale=1.5 ** 0.5)
-            nc.vector.tensor_tensor(out=n8[:, e, :], in0=a2[:], in1=h2[:], op=ALU.subtract)
-            w = tmpp.tile([P, HC], F32, tag="w")
-            nc.scalar.activation(out=w[:], in_=sv, func=ACT.Abs, bias=-10.0)
-            nc.scalar.activation(out=n9[:, e, :], in_=w[:], func=ACT.Relu, bias=1.0, scale=-1.0)
-            a2 = tmpp.tile([P, HC], F32, tag="a2")
-            nc.vector.tensor_scalar(out=a2[:], in0=sv, scalar1=11.0, scalar2=None, op0=ALU.is_lt)
-            nc.vector.scalar_tensor_tensor(out=n10[:, e, :], in0=sv, scalar=10.0, in1=a2[:], op0=ALU.is_ge, op1=ALU.mult)
-        quantise_plane(8, n8)
-        quantise_plane(9, n9)
-        quantise_plane(10, n10)
+            nc.vector.tensor_tensor(out=n8[:], in0=a2[:], in1=h2[:], op=ALU.subtract)
+            quantise_plane(8, h, n8)
 
-        acc = [[pacc.tile([P, 512], F32, tag="acc%d%d" % (h, q), name="acc%d%d" % (h, q)) for q in range(2)] for h in range(2)]
-        bias_bc = const.tile([P, OUT_F], BF16)
-        gamma_bc = const.tile([P, OUT_F], BF16)
-        beta_bc = const.tile([P, OUT_F], BF16)
-        PIECES = [(0, 8), (8, 16), (16, 20), (20, 22)]
-        evac_no = 0
-        for c in range(NCHUNK):
-            if c < 2:
-                raw = raws[c]
-            else:
-                raw = rawp.tile([P, IN_F * NK], BF16, tag="raw", name="raw%d" % c)
-                nc.sync.dma_start(out=raw[:], in_=cpv[c])
-            if c == 3:
-                nc.sync.dma_start(out=bias_bc[:], in_=b.partition_broadcast(P))
-                nc.sync.dma_start(out=gamma_bc[:], in_=gamma.partition_broadcast(P))
-                nc.sync.dma_start(out=beta_bc[:], in_=beta.partition_broadcast(P))
-            raww = raw[:].bitcast(F32)
-            cc = codp.tile([P, NSLOT, P], U32, tag="cc", align_bytes=64)
-            cs = codp.tile([P, NSLOT, P], U8, tag="cs", align_bytes=64)
-            for (f0, f1) in PIECES:
-                grp = grpp.tile([P, f1 - f0, P, 4], BF16, tag="grp", align_bytes=64)
-                for wd in range(f0 // 2, f1 // 2):
-                    pt = ptr.tile([P, 4, P], F32, tag="pt")
-                    for u in range(4):
-                        st = WORDS_Q * u + wd
-                        nc.tensor.transpose(pt[:, u, :], raww[:, st:st + NK * 127 + 1:NK], ident[:])
-                    src = pt[:].bitcast(BF16).rearrange("p u (o e) -> p e o u", e=2)
-                    dst = grp[:, 2 * wd - f0:2 * wd - f0 + 2, :, :]
-                    if evac_no % 2 == 0:
-                        nc.scalar.copy(out=dst, in_=src)
-                    else:
-                        nc.vector.tensor_copy(out=dst, in_=src)
-                    evac_no += 1
-                nc.vector.quantize_mx(
-                    out=cc[:, f0:f1, :].rearrange("p f o -> p (f o)").bitcast(FP8X4),
-                    scales=cs[:, f0:f1, :].rearrange("p f o -> p (f o)"),
-                    in_=grp[:].rearrange("p f o u -> p (f o u)"),
-                )
+        def low_unit_b(h):
+            xv = xp[:, h, :, :, :].rearrange("p e b u -> p (e b u)")
+            n9 = new_plane(9, h)
+            n10 = new_plane(10, h)
+            w = tmpp.tile([P, HC], F32, tag="w", name="w")
+            nc.scalar.activation(out=w[:], in_=xv, func=ACT.Abs, bias=-10.0, scale=11.0)
+            nc.scalar.activation(out=n9[:], in_=w[:], func=ACT.Relu, bias=1.0, scale=-1.0)
+            fb = tmpp.tile([P, HC], BF16, tag="fb", name="fb")
+            nc.vector.tensor_scalar(out=fb[:], in0=xv, scalar1=1.0, scalar2=None, op0=ALU.is_lt)
+            nc.vector.scalar_tensor_tensor(out=n10[:], in0=xv, scalar=10.0 / 11.0, in1=fb[:], op0=ALU.is_ge, op1=ALU.mult)
+            quantise_plane(9, h, n9)
+            quantise_plane(10, h, n10)
+
+        units = []
+        for rho in range(2):
             for h in range(2):
-                dst = acc[h][c // 4][:, (c % 4) * P:(c % 4 + 1) * P]
-                for f in range(NSLOT):
-                    par, k = divmod(f, NK)
-                    col = par * B + h * P
+                units.append(("cubic", rho, h, (rho, rho + 4)))
+        for h in range(2):
+            units.append(("low_a", 0, h, (8,)))
+        for h in range(2):
+            units.append(("low_b", 0, h, (9, 10)))
+        for rho in range(2, 4):
+            for h in range(2):
+                units.append(("cubic", rho, h, (rho, rho + 4)))
+        n_woven = len(units) - TRAIL
+        n_banks = NCHUNK * NK
+
+        plan = []
+        for g in range(2):
+            for h in range(2):
+                for q in range(2):
+                    plan.append(("lin", g, h, q))
+        ready = []
+        halves_done = 0
+
+        def plan_unit(unit):
+            plan.append(("unit", unit))
+            for k in unit[3]:
+                for q in range(halves_done):
+                    plan.append(("mx", k, unit[2], q))
+                ready.append((k, unit[2]))
+
+        plan_unit(units[0])
+        n_given = 1
+        for bank in range(n_banks):
+            c, wd = divmod(bank, NK)
+            plan.append(("bank", c, wd, bank))
+            if wd == NK - 1 and c % 4 == 3:
+                for (k, h) in ready:
+                    plan.append(("mx", k, h, halves_done))
+                halves_done += 1
+            if n_given < n_woven and (bank + 1) * (n_woven - 1) >= n_given * n_banks:
+                plan_unit(units[n_given])
+                n_given += 1
+        while n_given < len(units):
+            plan_unit(units[n_given])
+            n_given += 1
+        last = {}
+        for n, act in enumerate(plan):
+            if act[0] == "mx":
+                last[(act[2], act[3])] = n
+
+        ccodes = const.tile([P, 2, NSLOT, 512], U32, align_bytes=64)
+        cscales = const.tile([P, 2, NSLOT, 512], U8, align_bytes=64)
+        acc = [[pacc.tile([P, 512], F32, tag="acc%d%d" % (h, q), name="acc%d%d" % (h, q)) for q in range(2)] for h in range(2)]
+        given_s = 0
+        raw_of = {}
+        for n, act in enumerate(plan):
+            if act[0] == "lin":
+                g, h, q = act[1], act[2], act[3]
+                col = g * B + h * P
+                nc.tensor.matmul_mx(
+                    out=acc[h][q][:],
+                    lhsT=xcodes[:, col:col + P].bitcast(FP8X4),
+                    lhsT_scale=xscales[:, col:col + P],
+                    rhs=wt[:, g, 1024 * q:1024 * (q + 1)].bitcast(FP4X4),
+                    rhs_scale=ws[:, g, 512 * q:512 * (q + 1)],
+                    start=(g == 0),
+                    stop=False,
+                )
+            elif act[0] == "unit":
+                kind, rho, h = act[1][0], act[1][1], act[1][2]
+                if kind == "cubic":
+                    cubic_unit(rho, h)
+                elif kind == "low_a":
+                    low_unit_a(h)
+                else:
+                    low_unit_b(h)
+            elif act[0] == "mx":
+                k, h, q = act[1], act[2], act[3]
+                for par in range(2):
+                    f = par * NK + k
                     nc.tensor.matmul_mx(
-                        out=dst,
-                        lhsT=bcodes[:, k, col:col + P].bitcast(FP8X4),
-                        lhsT_scale=bscales[:, k, col:col + P],
-                        rhs=cc[:, f, :].bitcast(FP8X4),
-                        rhs_scale=cs[:, f, :],
-                        start=(f == 0),
-                        stop=False,
-                    )
-                for g in range(2):
-                    col = g * B + h * P
-                    nc.tensor.matmul_mx(
-                        out=dst,
-                        lhsT=xcodes[:, col:col + P].bitcast(FP8X4),
-                        lhsT_scale=xscales[:, col:col + P],
-                        rhs=wt[:, g, 2 * P * c:2 * P * (c + 1)].bitcast(FP4X4),
-                        rhs_scale=ws[:, g, P * c:P * (c + 1)],
+                        out=acc[h][q][:],
+                        lhsT=bcodes[:, k, h, par * P:(par + 1) * P].bitcast(FP8X4),
+                        lhsT_scale=bscales[:, k, h, par * P:(par + 1) * P],
+                        rhs=ccodes[:, q, f, :].bitcast(FP8X4),
+                        rhs_scale=cscales[:, q, f, :],
                         start=False,
-                        stop=(g == 1),
+                        stop=(par == 1 and last[(h, q)] == n),
+                    )
+            else:
+                c, wd, bank = act[1], act[2], act[3]
+                if wd == 0:
+                    if c < 2:
+                        raw_of[c] = raws[c]
+                    else:
+                        raw = rawp.tile([P, IN_F * NK], BF16, tag="raw", name="raw%d" % c)
+                        nc.sync.dma_start(out=raw[:], in_=cpv[c])
+                        raw_of[c] = raw
+                raww = raw_of[c][:].bitcast(F32)
+                pt = ptr.tile([P, 4, P], F32, tag="pt", name="pt")
+                for u in range(4):
+                    st = WORDS_Q * u + wd
+                    nc.tensor.transpose(pt[:, u, :], raww[:, st:st + NK * 127 + 1:NK], ident[:])
+                grp = grpp.tile([P, 2, P, 4], BF16, tag="grp", name="grp", align_bytes=64)
+                src = pt[:].bitcast(BF16).rearrange("p u (o e) -> p e o u", e=2)
+                if (bank + 1) * S_NUM // S_DEN > given_s:
+                    given_s += 1
+                    nc.scalar.copy(out=grp[:], in_=src)
+                else:
+                    nc.vector.tensor_copy(out=grp[:], in_=src)
+                q, c4 = divmod(c, 4)
+                for e in range(2):
+                    f = 2 * wd + e
+                    nc.vector.quantize_mx(
+                        out=ccodes[:, q, f, c4 * P:(c4 + 1) * P].bitcast(FP8X4),
+                        scales=cscales[:, q, f, c4 * P:(c4 + 1) * P],
+                        in_=grp[:, e, :, :].rearrange("p o u -> p (o u)"),
                     )
 
+        gb = rawp.tile([P, 3, OUT_F], BF16, tag="raw", name="gb")
+        nc.sync.dma_start(out=gb[:, 0, :], in_=b.partition_broadcast(P))
+        nc.sync.dma_start(out=gb[:, 1, :], in_=gamma.partition_broadcast(P))
+        nc.sync.dma_start(out=gb[:, 2, :], in_=beta.partition_broadcast(P))
+        yt = rawp.tile([P, 2, OUT_F], F32, tag="raw", name="yt")
         for h in range(2):
-            y = lnp.tile([P, OUT_F], F32, tag="y")
-            stats = lnp.tile([P, 2, 6], F32, tag="stats")
+            y = yt[:, h, :]
+            stats = lnp.tile([P, 2, 6], F32, tag="stats", name="stats")
             for q in range(2):
                 sl = slice(q * 512, (q + 1) * 512)
-                nc.vector.tensor_tensor(out=y[:, sl], in0=acc[h][q][:], in1=bias_bc[:, sl], op=ALU.add)
-                nc.vector.bn_stats(out=stats[:, q, :], in_=y[:, sl])
-            mv = lnp.tile([P, 2], F32, tag="mv")
+                nc.vector.tensor_tensor(out=yt[:, h, sl], in0=acc[h][q][:], in1=gb[:, 0, sl], op=ALU.add)
+                nc.vector.bn_stats(out=stats[:, q, :], in_=yt[:, h, sl])
+            mv = lnp.tile([P, 2], F32, tag="mv", name="mv")
             nc.vector.bn_aggr(out=mv[:], in_=stats[:].rearrange("p q s -> p (q s)"))
-            rstd = lnp.tile([P, 1], F32, tag="rstd")
+            rstd = lnp.tile([P, 1], F32, tag="rstd", name="rstd")
             nc.scalar.activation(out=rstd[:], in_=mv[:, 1:2], func=ACT.Sqrt, bias=EPS)
             nc.vector.reciprocal(out=rstd[:], in_=rstd[:])
-            nc.vector.tensor_scalar(out=y[:], in0=y[:], scalar1=mv[:, 0:1], scalar2=rstd[:], op0=ALU.subtract, op1=ALU.mult)
-            nc.vector.tensor_tensor(out=y[:], in0=y[:], in1=gamma_bc[:], op=ALU.mult)
-            nc.vector.tensor_tensor(out=y[:], in0=y[:], in1=beta_bc[:], op=ALU.add)
-            nc.sync.dma_start(out=out[h * P:(h + 1) * P, :], in_=y[:])
+            nc.vector.scalar_tensor_tensor(out=y, in0=y, scalar=mv[:, 0:1], in1=gb[:, 1, :], op0=ALU.subtract, op1=ALU.mult)
+            nc.vector.scalar_tensor_tensor(out=y, in0=y, scalar=rstd[:], in1=gb[:, 2, :], op0=ALU.mult, op1=ALU.add)
+            nc.sync.dma_start(out=out[h * P:(h + 1) * P, :], in_=y)

@@ -23,10 +23,15 @@ FLOPS = 2 * B * OUT_F * (IN_F * NK + IN_F)
 
 NCHUNK = OUT_F // P
 NSLOT = 2 * NK
+NBANK = NCHUNK * NK
 WORDS_Q = 128 * NK
 HC = 1024
-S_NUM, S_DEN = 15, 22
-TRAIL = 3
+S_NUM, S_DEN = 7, 10
+S_FIRST = 6
+PERIOD = 14
+QLAG = 2
+MAXA = 5
+C2 = (2.0 / 3.0) ** 0.5
 
 
 def tile_bsplinekan_kernel(tc, x, control_points, W_words, W_scales, b, gamma, beta, out):
@@ -40,17 +45,16 @@ def tile_bsplinekan_kernel(tc, x, control_points, W_words, W_scales, b, gamma, b
         lnp = ctx.enter_context(tc.tile_pool(name="lnp", bufs=2))
         pacc = ctx.enter_context(tc.psum_pool(name="pacc", bufs=1))
         ptr = ctx.enter_context(tc.psum_pool(name="ptr", bufs=4))
+        ctx.enter_context(tc.manual_schedule())
 
         x_sb = const.tile([P, 2, IN_F], BF16)
         nc.sync.dma_start(out=x_sb[:], in_=x.rearrange("(h p) i -> p h i", p=P))
-
         cpv = control_points.rearrange("(c p) i k -> c p (i k)", p=P)
-        raws = []
+        raw_of = {}
         for c in range(2):
             raw = rawp.tile([P, IN_F * NK], BF16, tag="raw", name="raw%d" % c)
             nc.sync.dma_start(out=raw[:], in_=cpv[c])
-            raws.append(raw)
-
+            raw_of[c] = raw
         ws = const.tile([P, 2, OUT_F], U8, align_bytes=64)
         nc.vector.memset(ws[:].bitcast(I32), 0)
         wt = const.tile([P, 2, 2 * OUT_F], U8, align_bytes=64)
@@ -61,7 +65,6 @@ def tile_bsplinekan_kernel(tc, x, control_points, W_words, W_scales, b, gamma, b
                 out=ws[r:P:32, :, :].bitcast(I32),
                 in_=wsv[:, r:16:4, :].rearrange("g q n -> q g n"),
             )
-
         ident = const.tile([P, P], F32)
         make_identity(nc, ident[:])
 
@@ -89,11 +92,13 @@ def tile_bsplinekan_kernel(tc, x, control_points, W_words, W_scales, b, gamma, b
             )
         xcodes = const.tile([P, 2 * B], U32, align_bytes=64)
         xscales = const.tile([P, 2 * B], U8, align_bytes=64)
-        nc.vector.quantize_mx(
-            out=xcodes[:].bitcast(FP8X4),
-            scales=xscales[:],
-            in_=xg[:].rearrange("p g b t -> p (g b t)"),
-        )
+
+        def quantise_x():
+            nc.vector.quantize_mx(
+                out=xcodes[:].bitcast(FP8X4),
+                scales=xscales[:],
+                in_=xg[:].rearrange("p g b t -> p (g b t)"),
+            )
 
         bcodes = const.tile([P, NK, 2, 2 * P], U32, align_bytes=64)
         bscales = const.tile([P, NK, 2, 2 * P], U8, align_bytes=64)
@@ -104,179 +109,273 @@ def tile_bsplinekan_kernel(tc, x, control_points, W_words, W_scales, b, gamma, b
         def quantise_plane(k, h, nb):
             nc.vector.quantize_mx(out=bcodes[:, k, h, :].bitcast(FP8X4), scales=bscales[:, k, h, :], in_=nb[:])
 
-        C2 = (2.0 / 3.0) ** 0.5
+        def x_view(h):
+            return xp[:, h, :, :, :].rearrange("p e b u -> p (e b u)")
 
         def cubic_unit(rho, h):
             mid = float(rho + 4)
-            xv = xp[:, h, :, :, :].rearrange("p e b u -> p (e b u)")
-            lo = new_plane(rho, h)
-            hi = new_plane(rho + 4, h)
-            w = tmpp.tile([P, HC], F32, tag="w", name="w")
-            nc.scalar.activation(out=w[:], in_=xv, func=ACT.Abs, bias=-mid, scale=11.0)
-            nc.scalar.activation(out=w[:], in_=w[:], func=ACT.Abs, bias=-2.0)
-            a2 = tmpp.tile([P, HC], F32, tag="a2", name="a2")
-            nc.scalar.activation(out=a2[:], in_=w[:], func=ACT.Square, bias=-2.0)
-            h2 = tmpp.tile([P, HC], F32, tag="h2", name="h2")
-            nc.scalar.activation(out=h2[:], in_=w[:], func=ACT.Square, bias=-C2, scale=C2)
-            nc.vector.scalar_tensor_tensor(out=a2[:], in0=w[:], scalar=2.0, in1=a2[:], op0=ALU.subtract, op1=ALU.mult)
-            nc.vector.scalar_tensor_tensor(out=h2[:], in0=w[:], scalar=1.0, in1=h2[:], op0=ALU.subtract, op1=ALU.mult)
-            nc.vector.tensor_scalar(out=a2[:], in0=a2[:], scalar1=0.0, scalar2=1.0 / 6.0, op0=ALU.min, op1=ALU.mult)
-            fb = tmpp.tile([P, HC], BF16, tag="fb", name="fb")
-            nc.vector.scalar_tensor_tensor(out=fb[:], in0=h2[:], scalar=0.0, in1=a2[:], op0=ALU.min, op1=ALU.subtract)
-            nc.vector.scalar_tensor_tensor(out=lo[:], in0=xv, scalar=mid / 11.0, in1=fb[:], op0=ALU.is_lt, op1=ALU.mult)
-            nc.vector.tensor_tensor(out=hi[:], in0=fb[:], in1=lo[:], op=ALU.subtract)
-            quantise_plane(rho, h, lo)
-            quantise_plane(rho + 4, h, hi)
+            xv = x_view(h)
+            t = {}
 
-        def low_unit_a(h):
-            xv = xp[:, h, :, :, :].rearrange("p e b u -> p (e b u)")
-            n8 = new_plane(8, h)
-            w = tmpp.tile([P, HC], F32, tag="w", name="w")
-            nc.scalar.activation(out=w[:], in_=xv, func=ACT.Abs, bias=-9.5, scale=11.0)
-            a2 = tmpp.tile([P, HC], F32, tag="a2", name="a2")
-            nc.vector.tensor_scalar(out=a2[:], in0=w[:], scalar1=1.5, scalar2=-1.5, op0=ALU.min, op1=ALU.add)
-            nc.scalar.activation(out=a2[:], in_=a2[:], func=ACT.Square, scale=0.5 ** 0.5)
-            h2 = tmpp.tile([P, HC], F32, tag="h2", name="h2")
-            nc.vector.tensor_scalar(out=h2[:], in0=w[:], scalar1=0.5, scalar2=-0.5, op0=ALU.min, op1=ALU.add)
-            nc.scalar.activation(out=h2[:], in_=h2[:], func=ACT.Square, scale=1.5 ** 0.5)
-            nc.vector.tensor_tensor(out=n8[:], in0=a2[:], in1=h2[:], op=ALU.subtract)
-            quantise_plane(8, h, n8)
+            def s0():
+                t["w"] = tmpp.tile([P, HC], F32, tag="w", name="w")
+                nc.scalar.activation(out=t["w"][:], in_=xv, func=ACT.Abs, bias=-mid, scale=11.0)
 
-        def low_unit_b(h):
-            xv = xp[:, h, :, :, :].rearrange("p e b u -> p (e b u)")
-            n9 = new_plane(9, h)
-            n10 = new_plane(10, h)
-            w = tmpp.tile([P, HC], F32, tag="w", name="w")
-            nc.scalar.activation(out=w[:], in_=xv, func=ACT.Abs, bias=-10.0, scale=11.0)
-            nc.scalar.activation(out=n9[:], in_=w[:], func=ACT.Relu, bias=1.0, scale=-1.0)
-            fb = tmpp.tile([P, HC], BF16, tag="fb", name="fb")
-            nc.vector.tensor_scalar(out=fb[:], in0=xv, scalar1=1.0, scalar2=None, op0=ALU.is_lt)
-            nc.vector.scalar_tensor_tensor(out=n10[:], in0=xv, scalar=10.0 / 11.0, in1=fb[:], op0=ALU.is_ge, op1=ALU.mult)
-            quantise_plane(9, h, n9)
-            quantise_plane(10, h, n10)
+            def s1():
+                nc.scalar.activation(out=t["w"][:], in_=t["w"][:], func=ACT.Abs, bias=-2.0)
 
-        units = []
-        for rho in range(2):
-            for h in range(2):
-                units.append(("cubic", rho, h, (rho, rho + 4)))
-        for h in range(2):
-            units.append(("low_a", 0, h, (8,)))
-        for h in range(2):
-            units.append(("low_b", 0, h, (9, 10)))
-        for rho in range(2, 4):
-            for h in range(2):
-                units.append(("cubic", rho, h, (rho, rho + 4)))
-        n_woven = len(units) - TRAIL
-        n_banks = NCHUNK * NK
+            def s2():
+                t["a"] = tmpp.tile([P, HC], F32, tag="a2", name="a2")
+                nc.scalar.activation(out=t["a"][:], in_=t["w"][:], func=ACT.Square, bias=-2.0)
 
-        plan = []
-        for g in range(2):
-            for h in range(2):
-                for q in range(2):
-                    plan.append(("lin", g, h, q))
-        ready = []
-        halves_done = 0
+            def s3():
+                t["h"] = tmpp.tile([P, HC], F32, tag="h2", name="h2")
+                nc.scalar.activation(out=t["h"][:], in_=t["w"][:], func=ACT.Square, bias=-C2, scale=C2)
 
-        def plan_unit(unit):
-            plan.append(("unit", unit))
-            for k in unit[3]:
-                for q in range(halves_done):
-                    plan.append(("mx", k, unit[2], q))
-                ready.append((k, unit[2]))
+            def v0():
+                nc.vector.scalar_tensor_tensor(out=t["a"][:], in0=t["w"][:], scalar=2.0, in1=t["a"][:], op0=ALU.subtract, op1=ALU.mult)
 
-        plan_unit(units[0])
-        n_given = 1
-        for bank in range(n_banks):
-            c, wd = divmod(bank, NK)
-            plan.append(("bank", c, wd, bank))
-            if wd == NK - 1 and c % 4 == 3:
-                for (k, h) in ready:
-                    plan.append(("mx", k, h, halves_done))
-                halves_done += 1
-            if n_given < n_woven and (bank + 1) * (n_woven - 1) >= n_given * n_banks:
-                plan_unit(units[n_given])
-                n_given += 1
-        while n_given < len(units):
-            plan_unit(units[n_given])
-            n_given += 1
-        last = {}
-        for n, act in enumerate(plan):
-            if act[0] == "mx":
-                last[(act[2], act[3])] = n
+            def v1():
+                nc.vector.scalar_tensor_tensor(out=t["h"][:], in0=t["w"][:], scalar=1.0, in1=t["h"][:], op0=ALU.subtract, op1=ALU.mult)
+
+            def v2():
+                nc.vector.tensor_scalar(out=t["a"][:], in0=t["a"][:], scalar1=0.0, scalar2=1.0 / 6.0, op0=ALU.min, op1=ALU.mult)
+
+            def v3():
+                t["f"] = tmpp.tile([P, HC], BF16, tag="fb", name="fb")
+                nc.vector.scalar_tensor_tensor(out=t["f"][:], in0=t["h"][:], scalar=0.0, in1=t["a"][:], op0=ALU.min, op1=ALU.subtract)
+
+            def v4():
+                t["lo"] = new_plane(rho, h)
+                nc.vector.scalar_tensor_tensor(out=t["lo"][:], in0=xv, scalar=mid / 11.0, in1=t["f"][:], op0=ALU.is_lt, op1=ALU.mult)
+
+            def v5():
+                t["hi"] = new_plane(rho + 4, h)
+                nc.vector.tensor_tensor(out=t["hi"][:], in0=t["f"][:], in1=t["lo"][:], op=ALU.subtract)
+
+            def v6():
+                quantise_plane(rho, h, t["lo"])
+
+            def v7():
+                quantise_plane(rho + 4, h, t["hi"])
+
+            return [("S", s0), ("S", s1), ("S", s2), ("S", s3), ("V", v0), ("V", v1), ("V", v2), ("V", v3),
+                    ("V", v4), ("V", v5), ("V", v6), ("V", v7)]
+
+        def low_unit_a(h, lt):
+            xv = x_view(h)
+            t = {}
+
+            def s0():
+                nc.scalar.activation(out=lt["w"], in_=xv, func=ACT.Abs, bias=-9.5, scale=11.0)
+
+            def v0():
+                nc.vector.tensor_scalar(out=lt["a"], in0=lt["w"], scalar1=1.5, scalar2=-1.5, op0=ALU.min, op1=ALU.add)
+
+            def v1():
+                nc.vector.tensor_scalar(out=lt["h"], in0=lt["w"], scalar1=0.5, scalar2=-0.5, op0=ALU.min, op1=ALU.add)
+
+            def s1():
+                nc.scalar.activation(out=lt["a"], in_=lt["a"], func=ACT.Square, scale=0.5 ** 0.5)
+
+            def s2():
+                nc.scalar.activation(out=lt["h"], in_=lt["h"], func=ACT.Square, scale=1.5 ** 0.5)
+
+            def v2():
+                t["n"] = new_plane(8, h)
+                nc.vector.tensor_tensor(out=t["n"][:], in0=lt["a"], in1=lt["h"], op=ALU.subtract)
+
+            def v3():
+                quantise_plane(8, h, t["n"])
+
+            return [("S", s0), ("V", v0), ("V", v1), ("S", s1), ("S", s2), ("V", v2), ("V", v3)]
+
+        def low_unit_b(h, lt):
+            xv = x_view(h)
+            t = {}
+
+            def s0():
+                nc.scalar.activation(out=lt["w"], in_=xv, func=ACT.Abs, bias=-10.0, scale=11.0)
+
+            def s1():
+                t["n9"] = new_plane(9, h)
+                nc.scalar.activation(out=t["n9"][:], in_=lt["w"], func=ACT.Relu, bias=1.0, scale=-1.0)
+
+            def v0():
+                nc.vector.tensor_scalar(out=lt["f"], in0=xv, scalar1=1.0, scalar2=None, op0=ALU.is_lt)
+
+            def v1():
+                t["n10"] = new_plane(10, h)
+                nc.vector.scalar_tensor_tensor(out=t["n10"][:], in0=xv, scalar=10.0 / 11.0, in1=lt["f"], op0=ALU.is_ge, op1=ALU.mult)
+
+            def v2():
+                quantise_plane(9, h, t["n9"])
+
+            def v3():
+                quantise_plane(10, h, t["n10"])
+
+            return [("S", s0), ("V", v0), ("S", s1), ("V", v1), ("V", v2), ("V", v3)]
 
         ccodes = const.tile([P, 2, NSLOT, 512], U32, align_bytes=64)
         cscales = const.tile([P, 2, NSLOT, 512], U8, align_bytes=64)
         acc = [[pacc.tile([P, 512], F32, tag="acc%d%d" % (h, q), name="acc%d%d" % (h, q)) for q in range(2)] for h in range(2)]
-        given_s = 0
-        raw_of = {}
-        for n, act in enumerate(plan):
-            if act[0] == "lin":
-                g, h, q = act[1], act[2], act[3]
-                col = g * B + h * P
+
+        def mx_action(e):
+            kind, a, h, q = e[1], e[2], e[3], e[4]
+            if kind == "lin":
+                col = a * B + h * P
                 nc.tensor.matmul_mx(
                     out=acc[h][q][:],
                     lhsT=xcodes[:, col:col + P].bitcast(FP8X4),
                     lhsT_scale=xscales[:, col:col + P],
-                    rhs=wt[:, g, 1024 * q:1024 * (q + 1)].bitcast(FP4X4),
-                    rhs_scale=ws[:, g, 512 * q:512 * (q + 1)],
-                    start=(g == 0),
+                    rhs=wt[:, a, 1024 * q:1024 * (q + 1)].bitcast(FP4X4),
+                    rhs_scale=ws[:, a, 512 * q:512 * (q + 1)],
+                    start=(a == 0),
                     stop=False,
                 )
-            elif act[0] == "unit":
-                kind, rho, h = act[1][0], act[1][1], act[1][2]
-                if kind == "cubic":
-                    cubic_unit(rho, h)
-                elif kind == "low_a":
-                    low_unit_a(h)
-                else:
-                    low_unit_b(h)
-            elif act[0] == "mx":
-                k, h, q = act[1], act[2], act[3]
+            else:
                 for par in range(2):
-                    f = par * NK + k
+                    f = par * NK + a
                     nc.tensor.matmul_mx(
                         out=acc[h][q][:],
-                        lhsT=bcodes[:, k, h, par * P:(par + 1) * P].bitcast(FP8X4),
-                        lhsT_scale=bscales[:, k, h, par * P:(par + 1) * P],
+                        lhsT=bcodes[:, a, h, par * P:(par + 1) * P].bitcast(FP8X4),
+                        lhsT_scale=bscales[:, a, h, par * P:(par + 1) * P],
                         rhs=ccodes[:, q, f, :].bitcast(FP8X4),
                         rhs_scale=cscales[:, q, f, :],
                         start=False,
-                        stop=(par == 1 and last[(h, q)] == n),
-                    )
-            else:
-                c, wd, bank = act[1], act[2], act[3]
-                if wd == 0:
-                    if c < 2:
-                        raw_of[c] = raws[c]
-                    else:
-                        raw = rawp.tile([P, IN_F * NK], BF16, tag="raw", name="raw%d" % c)
-                        nc.sync.dma_start(out=raw[:], in_=cpv[c])
-                        raw_of[c] = raw
-                raww = raw_of[c][:].bitcast(F32)
-                pt = ptr.tile([P, 4, P], F32, tag="pt", name="pt")
-                for u in range(4):
-                    st = WORDS_Q * u + wd
-                    nc.tensor.transpose(pt[:, u, :], raww[:, st:st + NK * 127 + 1:NK], ident[:])
-                grp = grpp.tile([P, 2, P, 4], BF16, tag="grp", name="grp", align_bytes=64)
-                src = pt[:].bitcast(BF16).rearrange("p u (o e) -> p e o u", e=2)
-                if (bank + 1) * S_NUM // S_DEN > given_s:
-                    given_s += 1
-                    nc.scalar.copy(out=grp[:], in_=src)
-                else:
-                    nc.vector.tensor_copy(out=grp[:], in_=src)
-                q, c4 = divmod(c, 4)
-                for e in range(2):
-                    f = 2 * wd + e
-                    nc.vector.quantize_mx(
-                        out=ccodes[:, q, f, c4 * P:(c4 + 1) * P].bitcast(FP8X4),
-                        scales=cscales[:, q, f, c4 * P:(c4 + 1) * P],
-                        in_=grp[:, e, :, :].rearrange("p o u -> p (o u)"),
+                        stop=(a == NK - 1 and par == 1),
                     )
 
-        gb = rawp.tile([P, 3, OUT_F], BF16, tag="raw", name="gb")
+        cp_ready = (4 * NK + QLAG + 2, NBANK + QLAG + 2)
+        mxq = []
+        for g in range(2):
+            for h in range(2):
+                for q in range(2):
+                    mxq.append((8, "lin", g, h, q))
+
+        def plane_ready(k, h, step):
+            for q in range(2):
+                mxq.append((max(step + 2, cp_ready[q]), "mx", k, h, q))
+
+        pt_of = {}
+        grp_of = {}
+
+        def transposes(n):
+            c, wd = divmod(n, NK)
+            if wd == 0 and c >= 2:
+                raw_of[c] = rawp.tile([P, IN_F * NK], BF16, tag="raw", name="raw%d" % c)
+                nc.sync.dma_start(out=raw_of[c][:], in_=cpv[c])
+            raww = raw_of[c][:].bitcast(F32)
+            pt_of[n] = ptr.tile([P, 4, P], F32, tag="pt", name="pt")
+            for u in range(4):
+                st = WORDS_Q * u + wd
+                nc.tensor.transpose(pt_of[n][:, u, :], raww[:, st:st + NK * 127 + 1:NK], ident[:])
+
+        def empty_bank(n, on_scalar):
+            grp_of[n] = grpp.tile([P, 2, P, 4], BF16, tag="grp", name="grp", align_bytes=64)
+            src = pt_of[n][:].bitcast(BF16).rearrange("p u (o e) -> p e o u", e=2)
+            if on_scalar:
+                nc.scalar.copy(out=grp_of[n][:], in_=src)
+            else:
+                nc.vector.tensor_copy(out=grp_of[n][:], in_=src)
+
+        def quantise_bank(n, e):
+            c, wd = divmod(n, NK)
+            q, c4 = divmod(c, 4)
+            f = 2 * wd + e
+            nc.vector.quantize_mx(
+                out=ccodes[:, q, f, c4 * P:(c4 + 1) * P].bitcast(FP8X4),
+                scales=cscales[:, q, f, c4 * P:(c4 + 1) * P],
+                in_=grp_of[n][:, e, :, :].rearrange("p o u -> p (o u)"),
+            )
+
+        on_s = []
+        given = 0
+        for n in range(NBANK):
+            if n < S_FIRST:
+                on_s.append(True)
+            elif (n - S_FIRST + 1) * S_NUM // S_DEN > given:
+                given += 1
+                on_s.append(True)
+            else:
+                on_s.append(False)
+
+        woven = [(0, 0), (0, 1), (1, 0), (1, 1), (2, 0), (2, 1), (3, 0)]
+        first = cubic_unit(0, 0)
+        for op in first[:4]:
+            op[1]()
+        quantise_x()
+        for op in first[4:]:
+            op[1]()
+        plane_ready(0, 0, 0)
+        plane_ready(4, 0, 0)
+
+        s_pend = []
+        v_pend = []
+        for n in range(NBANK + QLAG):
+            m, r = divmod(n - 2, PERIOD)
+            if n >= 2 and r == 0 and m + 1 < len(woven):
+                rho, h = woven[m + 1]
+                ops = cubic_unit(rho, h)
+                for j in range(4):
+                    s_pend.append((n + j, ops[j][1]))
+                for j in range(8):
+                    v_pend.append((n + 3 + j, ops[4 + j][1]))
+                plane_ready(rho, h, n + 9)
+                plane_ready(rho + 4, h, n + 10)
+            if n < NBANK and n % 4 == 0:
+                for n1 in range(n, n + 4):
+                    transposes(n1)
+                take = [e for e in mxq if e[0] <= n][:MAXA]
+                mxq = [e for e in mxq if e not in take]
+                for e in take:
+                    mx_action(e)
+            if n < NBANK and on_s[n]:
+                empty_bank(n, True)
+            if s_pend and s_pend[0][0] <= n:
+                s_pend.pop(0)[1]()
+            if n >= QLAG:
+                quantise_bank(n - QLAG, 0)
+            if v_pend and v_pend[0][0] <= n:
+                v_pend.pop(0)[1]()
+            if n >= QLAG:
+                quantise_bank(n - QLAG, 1)
+            if n < NBANK and not on_s[n]:
+                empty_bank(n, False)
+        for e in mxq:
+            mx_action(e)
+
+        x1 = rawp.tile([P, IN_F * NK], BF16, tag="raw", name="x1")
+        gb = x1[:, 0:3 * OUT_F].rearrange("p (a n) -> p a n", a=3)
         nc.sync.dma_start(out=gb[:, 0, :], in_=b.partition_broadcast(P))
         nc.sync.dma_start(out=gb[:, 1, :], in_=gamma.partition_broadcast(P))
         nc.sync.dma_start(out=gb[:, 2, :], in_=beta.partition_broadcast(P))
+        lt = {
+            "w": x1[:, 3072:5120].bitcast(F32),
+            "a": x1[:, 5120:7168].bitcast(F32),
+            "h": x1[:, 7168:9216].bitcast(F32),
+            "f": x1[:, 9216:10240],
+        }
+        side_a = cubic_unit(3, 1)
+        side_b = low_unit_a(0, lt) + low_unit_b(0, lt) + low_unit_a(1, lt) + low_unit_b(1, lt)
+        ia = 0
+        ib = 0
+        while ia < len(side_a) or ib < len(side_b):
+            for rep in range(2):
+                if ib < len(side_b):
+                    side_b[ib][1]()
+                    ib += 1
+            if ia < len(side_a):
+                side_a[ia][1]()
+                ia += 1
+        for (h, ks) in ((0, (8, 9, 10)), (1, (3, 7, 8, 9, 10))):
+            for k in ks:
+                for q in range(2):
+                    mx_action((0, "mx", k, h, q))
+
+        one = lnp.tile([P, 1], F32, tag="one", name="one")
+        nc.vector.memset(one[:], 1.0)
+        nc.scalar.activation(out=one[:], in_=one[:], func=ACT.Sqrt)
         yt = rawp.tile([P, 2, OUT_F], F32, tag="raw", name="yt")
         for h in range(2):
             y = yt[:, h, :]
@@ -284,6 +383,8 @@ def tile_bsplinekan_kernel(tc, x, control_points, W_words, W_scales, b, gamma, b
             for q in range(2):
                 sl = slice(q * 512, (q + 1) * 512)
                 nc.vector.tensor_tensor(out=yt[:, h, sl], in0=acc[h][q][:], in1=gb[:, 0, sl], op=ALU.add)
+            for q in range(2):
+                sl = slice(q * 512, (q + 1) * 512)
                 nc.vector.bn_stats(out=stats[:, q, :], in_=yt[:, h, sl])
             mv = lnp.tile([P, 2], F32, tag="mv", name="mv")
             nc.vector.bn_aggr(out=mv[:], in_=stats[:].rearrange("p q s -> p (q s)"))

@@ -23,15 +23,9 @@ FLOPS = 2 * B * OUT_F * (IN_F * NK + IN_F)
 
 NCHUNK = OUT_F // P
 NSLOT = 2 * NK
-NBANK = NCHUNK * NK
 WORDS_Q = 128 * NK
 HC = 1024
-S_NUM, S_DEN = 7, 10
-S_FIRST = 6
-PERIOD = 14
-QLAG = 2
-MAXA = 5
-C2 = (2.0 / 3.0) ** 0.5
+TRAIL = 3
 
 
 def tile_bsplinekan_kernel(tc, x, control_points, W_words, W_scales, b, gamma, beta, out):
@@ -45,16 +39,17 @@ def tile_bsplinekan_kernel(tc, x, control_points, W_words, W_scales, b, gamma, b
         lnp = ctx.enter_context(tc.tile_pool(name="lnp", bufs=2))
         pacc = ctx.enter_context(tc.psum_pool(name="pacc", bufs=1))
         ptr = ctx.enter_context(tc.psum_pool(name="ptr", bufs=4))
-        ctx.enter_context(tc.manual_schedule())
 
         x_sb = const.tile([P, 2, IN_F], BF16)
         nc.sync.dma_start(out=x_sb[:], in_=x.rearrange("(h p) i -> p h i", p=P))
+
         cpv = control_points.rearrange("(c p) i k -> c p (i k)", p=P)
-        raw_of = {}
+        raws = []
         for c in range(2):
             raw = rawp.tile([P, IN_F * NK], BF16, tag="raw", name="raw%d" % c)
             nc.sync.dma_start(out=raw[:], in_=cpv[c])
-            raw_of[c] = raw
+            raws.append(raw)
+
         ws = const.tile([P, 2, OUT_F], U8, align_bytes=64)
         nc.vector.memset(ws[:].bitcast(I32), 0)
         wt = const.tile([P, 2, 2 * OUT_F], U8, align_bytes=64)
@@ -65,6 +60,7 @@ def tile_bsplinekan_kernel(tc, x, control_points, W_words, W_scales, b, gamma, b
                 out=ws[r:P:32, :, :].bitcast(I32),
                 in_=wsv[:, r:16:4, :].rearrange("g q n -> q g n"),
             )
+
         ident = const.tile([P, P], F32)
         make_identity(nc, ident[:])
 
@@ -92,13 +88,11 @@ def tile_bsplinekan_kernel(tc, x, control_points, W_words, W_scales, b, gamma, b
             )
         xcodes = const.tile([P, 2 * B], U32, align_bytes=64)
         xscales = const.tile([P, 2 * B], U8, align_bytes=64)
-
-        def quantise_x():
-            nc.vector.quantize_mx(
-                out=xcodes[:].bitcast(FP8X4),
-                scales=xscales[:],
-                in_=xg[:].rearrange("p g b t -> p (g b t)"),
-            )
+        nc.vector.quantize_mx(
+            out=xcodes[:].bitcast(FP8X4),
+            scales=xscales[:],
+            in_=xg[:].rearrange("p g b t -> p (g b t)"),
+        )
 
         bcodes = const.tile([P, NK, 2, 2 * P], U32, align_bytes=64)
         bscales = const.tile([P, NK, 2, 2 * P], U8, align_bytes=64)
@@ -109,273 +103,174 @@ def tile_bsplinekan_kernel(tc, x, control_points, W_words, W_scales, b, gamma, b
         def quantise_plane(k, h, nb):
             nc.vector.quantize_mx(out=bcodes[:, k, h, :].bitcast(FP8X4), scales=bscales[:, k, h, :], in_=nb[:])
 
-        def x_view(h):
-            return xp[:, h, :, :, :].rearrange("p e b u -> p (e b u)")
+        C2 = (2.0 / 3.0) ** 0.5
 
         def cubic_unit(rho, h):
             mid = float(rho + 4)
-            xv = x_view(h)
-            t = {}
+            xv = xp[:, h, :, :, :].rearrange("p e b u -> p (e b u)")
+            lo = new_plane(rho, h)
+            hi = new_plane(rho + 4, h)
+            w = tmpp.tile([P, HC], F32, tag="w", name="w")
+            nc.scalar.activation(out=w[:], in_=xv, func=ACT.Abs, bias=-mid, scale=11.0)
+            nc.scalar.activation(out=w[:], in_=w[:], func=ACT.Abs, bias=-2.0)
+            a2 = tmpp.tile([P, HC], F32, tag="a2", name="a2")
+            nc.scalar.activation(out=a2[:], in_=w[:], func=ACT.Square, bias=-2.0)
+            h2 = tmpp.tile([P, HC], F32, tag="h2", name="h2")
+            nc.scalar.activation(out=h2[:], in_=w[:], func=ACT.Square, bias=-C2, scale=C2)
+            nc.vector.scalar_tensor_tensor(out=a2[:], in0=w[:], scalar=2.0, in1=a2[:], op0=ALU.subtract, op1=ALU.mult)
+            nc.vector.scalar_tensor_tensor(out=h2[:], in0=w[:], scalar=1.0, in1=h2[:], op0=ALU.subtract, op1=ALU.mult)
+            nc.vector.tensor_scalar(out=a2[:], in0=a2[:], scalar1=0.0, scalar2=1.0 / 6.0, op0=ALU.min, op1=ALU.mult)
+            fb = tmpp.tile([P, HC], BF16, tag="fb", name="fb")
+            nc.vector.scalar_tensor_tensor(out=fb[:], in0=h2[:], scalar=0.0, in1=a2[:], op0=ALU.min, op1=ALU.subtract)
+            nc.vector.scalar_tensor_tensor(out=lo[:], in0=xv, scalar=mid / 11.0, in1=fb[:], op0=ALU.is_lt, op1=ALU.mult)
+            nc.vector.tensor_tensor(out=hi[:], in0=fb[:], in1=lo[:], op=ALU.subtract)
+            quantise_plane(rho, h, lo)
+            quantise_plane(rho + 4, h, hi)
 
-            def s0():
-                t["w"] = tmpp.tile([P, HC], F32, tag="w", name="w")
-                nc.scalar.activation(out=t["w"][:], in_=xv, func=ACT.Abs, bias=-mid, scale=11.0)
+        def low_unit_a(h):
+            xv = xp[:, h, :, :, :].rearrange("p e b u -> p (e b u)")
+            n8 = new_plane(8, h)
+            w = tmpp.tile([P, HC], F32, tag="w", name="w")
+            nc.scalar.activation(out=w[:], in_=xv, func=ACT.Abs, bias=-9.5, scale=11.0)
+            a2 = tmpp.tile([P, HC], F32, tag="a2", name="a2")
+            nc.vector.tensor_scalar(out=a2[:], in0=w[:], scalar1=1.5, scalar2=-1.5, op0=ALU.min, op1=ALU.add)
+            nc.scalar.activation(out=a2[:], in_=a2[:], func=ACT.Square, scale=0.5 ** 0.5)
+            h2 = tmpp.tile([P, HC], F32, tag="h2", name="h2")
+            nc.vector.tensor_scalar(out=h2[:], in0=w[:], scalar1=0.5, scalar2=-0.5, op0=ALU.min, op1=ALU.add)
+            nc.scalar.activation(out=h2[:], in_=h2[:], func=ACT.Square, scale=1.5 ** 0.5)
+            nc.vector.tensor_tensor(out=n8[:], in0=a2[:], in1=h2[:], op=ALU.subtract)
+            quantise_plane(8, h, n8)
 
-            def s1():
-                nc.scalar.activation(out=t["w"][:], in_=t["w"][:], func=ACT.Abs, bias=-2.0)
+        def low_unit_b(h):
+            xv = xp[:, h, :, :, :].rearrange("p e b u -> p (e b u)")
+            n9 = new_plane(9, h)
+            n10 = new_plane(10, h)
+            w = tmpp.tile([P, HC], F32, tag="w", name="w")
+            nc.scalar.activation(out=w[:], in_=xv, func=ACT.Abs, bias=-10.0, scale=11.0)
+            nc.scalar.activation(out=n9[:], in_=w[:], func=ACT.Relu, bias=1.0, scale=-1.0)
+            fb = tmpp.tile([P, HC], BF16, tag="fb", name="fb")
+            nc.vector.tensor_scalar(out=fb[:], in0=xv, scalar1=1.0, scalar2=None, op0=ALU.is_lt)
+            nc.vector.scalar_tensor_tensor(out=n10[:], in0=xv, scalar=10.0 / 11.0, in1=fb[:], op0=ALU.is_ge, op1=ALU.mult)
+            quantise_plane(9, h, n9)
+            quantise_plane(10, h, n10)
 
-            def s2():
-                t["a"] = tmpp.tile([P, HC], F32, tag="a2", name="a2")
-                nc.scalar.activation(out=t["a"][:], in_=t["w"][:], func=ACT.Square, bias=-2.0)
+        units = []
+        for rho in range(2):
+            for h in range(2):
+                units.append(("cubic", rho, h, (rho, rho + 4)))
+        for h in range(2):
+            units.append(("low_a", 0, h, (8,)))
+        for h in range(2):
+            units.append(("low_b", 0, h, (9, 10)))
+        for rho in range(2, 4):
+            for h in range(2):
+                units.append(("cubic", rho, h, (rho, rho + 4)))
+        n_woven = len(units) - TRAIL
+        n_banks = NCHUNK * NK
 
-            def s3():
-                t["h"] = tmpp.tile([P, HC], F32, tag="h2", name="h2")
-                nc.scalar.activation(out=t["h"][:], in_=t["w"][:], func=ACT.Square, bias=-C2, scale=C2)
+        plan = []
+        for g in range(2):
+            for h in range(2):
+                for q in range(2):
+                    plan.append(("lin", g, h, q))
+        ready = []
+        halves_done = 0
 
-            def v0():
-                nc.vector.scalar_tensor_tensor(out=t["a"][:], in0=t["w"][:], scalar=2.0, in1=t["a"][:], op0=ALU.subtract, op1=ALU.mult)
+        def plan_unit(unit):
+            plan.append(("unit", unit))
+            for k in unit[3]:
+                for q in range(halves_done):
+                    plan.append(("mx", k, unit[2], q))
+                ready.append((k, unit[2]))
 
-            def v1():
-                nc.vector.scalar_tensor_tensor(out=t["h"][:], in0=t["w"][:], scalar=1.0, in1=t["h"][:], op0=ALU.subtract, op1=ALU.mult)
-
-            def v2():
-                nc.vector.tensor_scalar(out=t["a"][:], in0=t["a"][:], scalar1=0.0, scalar2=1.0 / 6.0, op0=ALU.min, op1=ALU.mult)
-
-            def v3():
-                t["f"] = tmpp.tile([P, HC], BF16, tag="fb", name="fb")
-                nc.vector.scalar_tensor_tensor(out=t["f"][:], in0=t["h"][:], scalar=0.0, in1=t["a"][:], op0=ALU.min, op1=ALU.subtract)
-
-            def v4():
-                t["lo"] = new_plane(rho, h)
-                nc.vector.scalar_tensor_tensor(out=t["lo"][:], in0=xv, scalar=mid / 11.0, in1=t["f"][:], op0=ALU.is_lt, op1=ALU.mult)
-
-            def v5():
-                t["hi"] = new_plane(rho + 4, h)
-                nc.vector.tensor_tensor(out=t["hi"][:], in0=t["f"][:], in1=t["lo"][:], op=ALU.subtract)
-
-            def v6():
-                quantise_plane(rho, h, t["lo"])
-
-            def v7():
-                quantise_plane(rho + 4, h, t["hi"])
-
-            return [("S", s0), ("S", s1), ("S", s2), ("S", s3), ("V", v0), ("V", v1), ("V", v2), ("V", v3),
-                    ("V", v4), ("V", v5), ("V", v6), ("V", v7)]
-
-        def low_unit_a(h, lt):
-            xv = x_view(h)
-            t = {}
-
-            def s0():
-                nc.scalar.activation(out=lt["w"], in_=xv, func=ACT.Abs, bias=-9.5, scale=11.0)
-
-            def v0():
-                nc.vector.tensor_scalar(out=lt["a"], in0=lt["w"], scalar1=1.5, scalar2=-1.5, op0=ALU.min, op1=ALU.add)
-
-            def v1():
-                nc.vector.tensor_scalar(out=lt["h"], in0=lt["w"], scalar1=0.5, scalar2=-0.5, op0=ALU.min, op1=ALU.add)
-
-            def s1():
-                nc.scalar.activation(out=lt["a"], in_=lt["a"], func=ACT.Square, scale=0.5 ** 0.5)
-
-            def s2():
-                nc.scalar.activation(out=lt["h"], in_=lt["h"], func=ACT.Square, scale=1.5 ** 0.5)
-
-            def v2():
-                t["n"] = new_plane(8, h)
-                nc.vector.tensor_tensor(out=t["n"][:], in0=lt["a"], in1=lt["h"], op=ALU.subtract)
-
-            def v3():
-                quantise_plane(8, h, t["n"])
-
-            return [("S", s0), ("V", v0), ("V", v1), ("S", s1), ("S", s2), ("V", v2), ("V", v3)]
-
-        def low_unit_b(h, lt):
-            xv = x_view(h)
-            t = {}
-
-            def s0():
-                nc.scalar.activation(out=lt["w"], in_=xv, func=ACT.Abs, bias=-10.0, scale=11.0)
-
-            def s1():
-                t["n9"] = new_plane(9, h)
-                nc.scalar.activation(out=t["n9"][:], in_=lt["w"], func=ACT.Relu, bias=1.0, scale=-1.0)
-
-            def v0():
-                nc.vector.tensor_scalar(out=lt["f"], in0=xv, scalar1=1.0, scalar2=None, op0=ALU.is_lt)
-
-            def v1():
-                t["n10"] = new_plane(10, h)
-                nc.vector.scalar_tensor_tensor(out=t["n10"][:], in0=xv, scalar=10.0 / 11.0, in1=lt["f"], op0=ALU.is_ge, op1=ALU.mult)
-
-            def v2():
-                quantise_plane(9, h, t["n9"])
-
-            def v3():
-                quantise_plane(10, h, t["n10"])
-
-            return [("S", s0), ("V", v0), ("S", s1), ("V", v1), ("V", v2), ("V", v3)]
+        plan_unit(units[0])
+        n_given = 1
+        for bank in range(n_banks):
+            c, wd = divmod(bank, NK)
+            plan.append(("bank", c, wd, bank))
+            if wd == NK - 1 and c % 4 == 3:
+                for (k, h) in ready:
+                    plan.append(("mx", k, h, halves_done))
+                halves_done += 1
+            if n_given < n_woven and (bank + 1) * (n_woven - 1) >= n_given * n_banks:
+                plan_unit(units[n_given])
+                n_given += 1
+        while n_given < len(units):
+            plan_unit(units[n_given])
+            n_given += 1
+        last = {}
+        for n, act in enumerate(plan):
+            if act[0] == "mx":
+                last[(act[2], act[3])] = n
 
         ccodes = const.tile([P, 2, NSLOT, 512], U32, align_bytes=64)
         cscales = const.tile([P, 2, NSLOT, 512], U8, align_bytes=64)
         acc = [[pacc.tile([P, 512], F32, tag="acc%d%d" % (h, q), name="acc%d%d" % (h, q)) for q in range(2)] for h in range(2)]
-
-        def mx_action(e):
-            kind, a, h, q = e[1], e[2], e[3], e[4]
-            if kind == "lin":
-                col = a * B + h * P
+        raw_of = {}
+        for n, act in enumerate(plan):
+            if act[0] == "lin":
+                g, h, q = act[1], act[2], act[3]
+                col = g * B + h * P
                 nc.tensor.matmul_mx(
                     out=acc[h][q][:],
                     lhsT=xcodes[:, col:col + P].bitcast(FP8X4),
                     lhsT_scale=xscales[:, col:col + P],
-                    rhs=wt[:, a, 1024 * q:1024 * (q + 1)].bitcast(FP4X4),
-                    rhs_scale=ws[:, a, 512 * q:512 * (q + 1)],
-                    start=(a == 0),
+                    rhs=wt[:, g, 1024 * q:1024 * (q + 1)].bitcast(FP4X4),
+                    rhs_scale=ws[:, g, 512 * q:512 * (q + 1)],
+                    start=(g == 0),
                     stop=False,
                 )
-            else:
+            elif act[0] == "unit":
+                kind, rho, h = act[1][0], act[1][1], act[1][2]
+                if kind == "cubic":
+                    cubic_unit(rho, h)
+                elif kind == "low_a":
+                    low_unit_a(h)
+                else:
+                    low_unit_b(h)
+            elif act[0] == "mx":
+                k, h, q = act[1], act[2], act[3]
                 for par in range(2):
-                    f = par * NK + a
+                    f = par * NK + k
                     nc.tensor.matmul_mx(
                         out=acc[h][q][:],
-                        lhsT=bcodes[:, a, h, par * P:(par + 1) * P].bitcast(FP8X4),
-                        lhsT_scale=bscales[:, a, h, par * P:(par + 1) * P],
+                        lhsT=bcodes[:, k, h, par * P:(par + 1) * P].bitcast(FP8X4),
+                        lhsT_scale=bscales[:, k, h, par * P:(par + 1) * P],
                         rhs=ccodes[:, q, f, :].bitcast(FP8X4),
                         rhs_scale=cscales[:, q, f, :],
                         start=False,
-                        stop=(a == NK - 1 and par == 1),
+                        stop=(par == 1 and last[(h, q)] == n),
+                    )
+            else:
+                c, wd, bank = act[1], act[2], act[3]
+                if wd == 0:
+                    if c < 2:
+                        raw_of[c] = raws[c]
+                    else:
+                        raw = rawp.tile([P, IN_F * NK], BF16, tag="raw", name="raw%d" % c)
+                        nc.sync.dma_start(out=raw[:], in_=cpv[c])
+                        raw_of[c] = raw
+                raww = raw_of[c][:].bitcast(F32)
+                pt = ptr.tile([P, 4, P], F32, tag="pt", name="pt")
+                for u in range(4):
+                    st = WORDS_Q * u + wd
+                    nc.tensor.transpose(pt[:, u, :], raww[:, st:st + NK * 127 + 1:NK], ident[:])
+                grp = grpp.tile([P, 2, P, 4], BF16, tag="grp", name="grp", align_bytes=64)
+                src = pt[:].bitcast(BF16).rearrange("p u (o e) -> p e o u", e=2)
+                nc.any.tensor_copy(out=grp[:], in_=src)
+                q, c4 = divmod(c, 4)
+                for e in range(2):
+                    f = 2 * wd + e
+                    nc.vector.quantize_mx(
+                        out=ccodes[:, q, f, c4 * P:(c4 + 1) * P].bitcast(FP8X4),
+                        scales=cscales[:, q, f, c4 * P:(c4 + 1) * P],
+                        in_=grp[:, e, :, :].rearrange("p o u -> p (o u)"),
                     )
 
-        cp_ready = (4 * NK + QLAG + 2, NBANK + QLAG + 2)
-        mxq = []
-        for g in range(2):
-            for h in range(2):
-                for q in range(2):
-                    mxq.append((8, "lin", g, h, q))
-
-        def plane_ready(k, h, step):
-            for q in range(2):
-                mxq.append((max(step + 2, cp_ready[q]), "mx", k, h, q))
-
-        pt_of = {}
-        grp_of = {}
-
-        def transposes(n):
-            c, wd = divmod(n, NK)
-            if wd == 0 and c >= 2:
-                raw_of[c] = rawp.tile([P, IN_F * NK], BF16, tag="raw", name="raw%d" % c)
-                nc.sync.dma_start(out=raw_of[c][:], in_=cpv[c])
-            raww = raw_of[c][:].bitcast(F32)
-            pt_of[n] = ptr.tile([P, 4, P], F32, tag="pt", name="pt")
-            for u in range(4):
-                st = WORDS_Q * u + wd
-                nc.tensor.transpose(pt_of[n][:, u, :], raww[:, st:st + NK * 127 + 1:NK], ident[:])
-
-        def empty_bank(n, on_scalar):
-            grp_of[n] = grpp.tile([P, 2, P, 4], BF16, tag="grp", name="grp", align_bytes=64)
-            src = pt_of[n][:].bitcast(BF16).rearrange("p u (o e) -> p e o u", e=2)
-            if on_scalar:
-                nc.scalar.copy(out=grp_of[n][:], in_=src)
-            else:
-                nc.vector.tensor_copy(out=grp_of[n][:], in_=src)
-
-        def quantise_bank(n, e):
-            c, wd = divmod(n, NK)
-            q, c4 = divmod(c, 4)
-            f = 2 * wd + e
-            nc.vector.quantize_mx(
-                out=ccodes[:, q, f, c4 * P:(c4 + 1) * P].bitcast(FP8X4),
-                scales=cscales[:, q, f, c4 * P:(c4 + 1) * P],
-                in_=grp_of[n][:, e, :, :].rearrange("p o u -> p (o u)"),
-            )
-
-        on_s = []
-        given = 0
-        for n in range(NBANK):
-            if n < S_FIRST:
-                on_s.append(True)
-            elif (n - S_FIRST + 1) * S_NUM // S_DEN > given:
-                given += 1
-                on_s.append(True)
-            else:
-                on_s.append(False)
-
-        woven = [(0, 0), (0, 1), (1, 0), (1, 1), (2, 0), (2, 1), (3, 0)]
-        first = cubic_unit(0, 0)
-        for op in first[:4]:
-            op[1]()
-        quantise_x()
-        for op in first[4:]:
-            op[1]()
-        plane_ready(0, 0, 0)
-        plane_ready(4, 0, 0)
-
-        s_pend = []
-        v_pend = []
-        for n in range(NBANK + QLAG):
-            m, r = divmod(n - 2, PERIOD)
-            if n >= 2 and r == 0 and m + 1 < len(woven):
-                rho, h = woven[m + 1]
-                ops = cubic_unit(rho, h)
-                for j in range(4):
-                    s_pend.append((n + j, ops[j][1]))
-                for j in range(8):
-                    v_pend.append((n + 3 + j, ops[4 + j][1]))
-                plane_ready(rho, h, n + 9)
-                plane_ready(rho + 4, h, n + 10)
-            if n < NBANK and n % 4 == 0:
-                for n1 in range(n, n + 4):
-                    transposes(n1)
-                take = [e for e in mxq if e[0] <= n][:MAXA]
-                mxq = [e for e in mxq if e not in take]
-                for e in take:
-                    mx_action(e)
-            if n < NBANK and on_s[n]:
-                empty_bank(n, True)
-            if s_pend and s_pend[0][0] <= n:
-                s_pend.pop(0)[1]()
-            if n >= QLAG:
-                quantise_bank(n - QLAG, 0)
-            if v_pend and v_pend[0][0] <= n:
-                v_pend.pop(0)[1]()
-            if n >= QLAG:
-                quantise_bank(n - QLAG, 1)
-            if n < NBANK and not on_s[n]:
-                empty_bank(n, False)
-        for e in mxq:
-            mx_action(e)
-
-        x1 = rawp.tile([P, IN_F * NK], BF16, tag="raw", name="x1")
-        gb = x1[:, 0:3 * OUT_F].rearrange("p (a n) -> p a n", a=3)
+        gb = rawp.tile([P, 3, OUT_F], BF16, tag="raw", name="gb")
         nc.sync.dma_start(out=gb[:, 0, :], in_=b.partition_broadcast(P))
         nc.sync.dma_start(out=gb[:, 1, :], in_=gamma.partition_broadcast(P))
         nc.sync.dma_start(out=gb[:, 2, :], in_=beta.partition_broadcast(P))
-        lt = {
-            "w": x1[:, 3072:5120].bitcast(F32),
-            "a": x1[:, 5120:7168].bitcast(F32),
-            "h": x1[:, 7168:9216].bitcast(F32),
-            "f": x1[:, 9216:10240],
-        }
-        side_a = cubic_unit(3, 1)
-        side_b = low_unit_a(0, lt) + low_unit_b(0, lt) + low_unit_a(1, lt) + low_unit_b(1, lt)
-        ia = 0
-        ib = 0
-        while ia < len(side_a) or ib < len(side_b):
-            for rep in range(2):
-                if ib < len(side_b):
-                    side_b[ib][1]()
-                    ib += 1
-            if ia < len(side_a):
-                side_a[ia][1]()
-                ia += 1
-        for (h, ks) in ((0, (8, 9, 10)), (1, (3, 7, 8, 9, 10))):
-            for k in ks:
-                for q in range(2):
-                    mx_action((0, "mx", k, h, q))
-
-        one = lnp.tile([P, 1], F32, tag="one", name="one")
-        nc.vector.memset(one[:], 1.0)
-        nc.scalar.activation(out=one[:], in_=one[:], func=ACT.Sqrt)
         yt = rawp.tile([P, 2, OUT_F], F32, tag="raw", name="yt")
         for h in range(2):
             y = yt[:, h, :]
@@ -383,8 +278,6 @@ def tile_bsplinekan_kernel(tc, x, control_points, W_words, W_scales, b, gamma, b
             for q in range(2):
                 sl = slice(q * 512, (q + 1) * 512)
                 nc.vector.tensor_tensor(out=yt[:, h, sl], in0=acc[h][q][:], in1=gb[:, 0, sl], op=ALU.add)
-            for q in range(2):
-                sl = slice(q * 512, (q + 1) * 512)
                 nc.vector.bn_stats(out=stats[:, q, :], in_=yt[:, h, sl])
             mv = lnp.tile([P, 2], F32, tag="mv", name="mv")
             nc.vector.bn_aggr(out=mv[:], in_=stats[:].rearrange("p q s -> p (q s)"))

@@ -25,7 +25,9 @@ NCHUNK = OUT_F // P
 NSLOT = 2 * NK
 WORDS_Q = 128 * NK
 HC = 1024
-TRAIL = 3
+TRAIL = 4
+MX_EVERY = 2
+MX_RUN = 2
 
 
 def tile_bsplinekan_kernel(tc, x, control_points, W_words, W_scales, b, gamma, beta, out):
@@ -35,64 +37,66 @@ def tile_bsplinekan_kernel(tc, x, control_points, W_words, W_scales, b, gamma, b
         rawp = ctx.enter_context(tc.tile_pool(name="rawp", bufs=2))
         grpp = ctx.enter_context(tc.tile_pool(name="grpp", bufs=4))
         tmpp = ctx.enter_context(tc.tile_pool(name="tmpp", bufs=1))
-        nbp = ctx.enter_context(tc.tile_pool(name="nbp", bufs=4))
         lnp = ctx.enter_context(tc.tile_pool(name="lnp", bufs=2))
         pacc = ctx.enter_context(tc.psum_pool(name="pacc", bufs=1))
         ptr = ctx.enter_context(tc.psum_pool(name="ptr", bufs=4))
 
-        x_sb = const.tile([P, 2, IN_F], BF16)
-        nc.sync.dma_start(out=x_sb[:], in_=x.rearrange("(h p) i -> p h i", p=P))
+        with tc.tile_pool(name="xin", bufs=1) as xin:
+            x_sb = xin.tile([P, 2, IN_F], BF16)
+            nc.sync.dma_start(out=x_sb[:], in_=x.rearrange("(h p) i -> p h i", p=P))
 
-        cpv = control_points.rearrange("(c p) i k -> c p (i k)", p=P)
-        raws = []
-        for c in range(2):
-            raw = rawp.tile([P, IN_F * NK], BF16, tag="raw", name="raw%d" % c)
-            nc.sync.dma_start(out=raw[:], in_=cpv[c])
-            raws.append(raw)
+            cpv = control_points.rearrange("(c p) i k -> c p (i k)", p=P)
+            raws = []
+            for c in range(2):
+                raw = rawp.tile([P, IN_F * NK], BF16, tag="raw", name="raw%d" % c)
+                nc.sync.dma_start(out=raw[:], in_=cpv[c])
+                raws.append(raw)
 
-        ws = const.tile([P, 2, OUT_F], U8, align_bytes=64)
-        nc.vector.memset(ws[:].bitcast(I32), 0)
-        wt = const.tile([P, 2, 2 * OUT_F], U8, align_bytes=64)
-        nc.sync.dma_start(out=wt[:].bitcast(I32), in_=W_words.bitcast(I32).rearrange("g p n -> p g n"))
-        wsv = W_scales.bitcast(I32)
-        for r in range(4):
-            nc.sync.dma_start(
-                out=ws[r:P:32, :, :].bitcast(I32),
-                in_=wsv[:, r:16:4, :].rearrange("g q n -> q g n"),
+            ws = const.tile([P, 2, OUT_F], U8, align_bytes=64)
+            nc.vector.memset(ws[:].bitcast(I32), 0)
+            wt = const.tile([P, 2, 2 * OUT_F], U8, align_bytes=64)
+            nc.sync.dma_start(out=wt[:].bitcast(I32), in_=W_words.bitcast(I32).rearrange("g p n -> p g n"))
+            wsv = W_scales.bitcast(I32)
+            for r in range(4):
+                nc.sync.dma_start(
+                    out=ws[r:P:32, :, :].bitcast(I32),
+                    in_=wsv[:, r:16:4, :].rearrange("g q n -> q g n"),
+                )
+
+            ident = const.tile([P, P], F32)
+            make_identity(nc, ident[:])
+
+            xp = const.tile([P, 2, 2, P, 4], BF16)
+            xg = xin.tile([P, 2, B, 4], BF16, align_bytes=64)
+            for h in range(2):
+                xw = x_sb[:, h, :].bitcast(F32)
+                pxs = ptr.tile([P, 4, P], F32, tag="pt", name="pxs%d" % h)
+                for u in range(4):
+                    nc.tensor.transpose(pxs[:, u, :], xw[:, P * u:P * (u + 1)], ident[:])
+                src = pxs[:].bitcast(BF16).rearrange("p u (b e) -> p e b u", e=2)
+                if h == 0:
+                    nc.scalar.copy(out=xp[:, h, :, :, :], in_=src)
+                else:
+                    nc.vector.tensor_copy(out=xp[:, h, :, :, :], in_=src)
+            for h in range(2):
+                xw = x_sb[:, h, :].bitcast(F32)
+                pxl = ptr.tile([P, 4, P], F32, tag="pt", name="pxl%d" % h)
+                for g in range(2):
+                    for u in range(2):
+                        nc.tensor.transpose(pxl[:, 2 * g + u, :], xw[:, 256 * g + u:256 * (g + 1):2], ident[:])
+                nc.vector.tensor_copy(
+                    out=xg[:, :, h * P:(h + 1) * P, :].bitcast(F32),
+                    in_=pxl[:].rearrange("p (g u) b -> p g b u", u=2),
+                )
+            xcodes = const.tile([P, 2 * B], U32, align_bytes=64)
+            xscales = const.tile([P, 2 * B], U8, align_bytes=64)
+            nc.vector.quantize_mx(
+                out=xcodes[:].bitcast(FP8X4),
+                scales=xscales[:],
+                in_=xg[:].rearrange("p g b t -> p (g b t)"),
             )
 
-        ident = const.tile([P, P], F32)
-        make_identity(nc, ident[:])
-
-        xp = const.tile([P, 2, 2, P, 4], BF16)
-        xg = const.tile([P, 2, B, 4], BF16, align_bytes=64)
-        for h in range(2):
-            xw = x_sb[:, h, :].bitcast(F32)
-            pxs = ptr.tile([P, 4, P], F32, tag="pt", name="pxs%d" % h)
-            for u in range(4):
-                nc.tensor.transpose(pxs[:, u, :], xw[:, P * u:P * (u + 1)], ident[:])
-            src = pxs[:].bitcast(BF16).rearrange("p u (b e) -> p e b u", e=2)
-            if h == 0:
-                nc.scalar.copy(out=xp[:, h, :, :, :], in_=src)
-            else:
-                nc.vector.tensor_copy(out=xp[:, h, :, :, :], in_=src)
-        for h in range(2):
-            xw = x_sb[:, h, :].bitcast(F32)
-            pxl = ptr.tile([P, 4, P], F32, tag="pt", name="pxl%d" % h)
-            for g in range(2):
-                for u in range(2):
-                    nc.tensor.transpose(pxl[:, 2 * g + u, :], xw[:, 256 * g + u:256 * (g + 1):2], ident[:])
-            nc.vector.tensor_copy(
-                out=xg[:, :, h * P:(h + 1) * P, :].bitcast(F32),
-                in_=pxl[:].rearrange("p (g u) b -> p g b u", u=2),
-            )
-        xcodes = const.tile([P, 2 * B], U32, align_bytes=64)
-        xscales = const.tile([P, 2 * B], U8, align_bytes=64)
-        nc.vector.quantize_mx(
-            out=xcodes[:].bitcast(FP8X4),
-            scales=xscales[:],
-            in_=xg[:].rearrange("p g b t -> p (g b t)"),
-        )
+        nbp = ctx.enter_context(tc.tile_pool(name="nbp", bufs=5))
 
         bcodes = const.tile([P, NK, 2, 2 * P], U32, align_bytes=64)
         bscales = const.tile([P, NK, 2, 2 * P], U8, align_bytes=64)
@@ -105,32 +109,51 @@ def tile_bsplinekan_kernel(tc, x, control_points, W_words, W_scales, b, gamma, b
 
         C2 = (2.0 / 3.0) ** 0.5
 
-        def cubic_unit(rho, h):
-            mid = float(rho + 4)
+        C1 = (1.0 / 6.0) ** 0.5
+
+        def pair_unit(rho, h):
             xv = xp[:, h, :, :, :].rearrange("p e b u -> p (e b u)")
-            lo = new_plane(rho, h)
-            hi = new_plane(rho + 4, h)
-            w = tmpp.tile([P, HC], F32, tag="w", name="w")
-            nc.scalar.activation(out=w[:], in_=xv, func=ACT.Abs, bias=-mid, scale=11.0)
-            nc.scalar.activation(out=w[:], in_=w[:], func=ACT.Abs, bias=-2.0)
+            cen = float(rho + 6)
+            y1 = tmpp.tile([P, HC], F32, tag="y1", name="y1")
+            nc.scalar.activation(out=y1[:], in_=xv, func=ACT.Abs, bias=-cen, scale=11.0)
+            tw = tmpp.tile([P, HC], F32, tag="tw", name="tw")
+            nc.scalar.activation(out=tw[:], in_=y1[:], func=ACT.Abs, bias=-4.0)
+            nc.scalar.activation(out=tw[:], in_=tw[:], func=ACT.Abs, bias=-2.0)
             a2 = tmpp.tile([P, HC], F32, tag="a2", name="a2")
-            nc.scalar.activation(out=a2[:], in_=w[:], func=ACT.Square, bias=-2.0)
+            nc.scalar.activation(out=a2[:], in_=tw[:], func=ACT.Square, scale=C1)
+            b2 = tmpp.tile([P, HC], F32, tag="b2", name="b2")
+            nc.scalar.activation(out=b2[:], in_=tw[:], func=ACT.Square, bias=-2.0 * C1, scale=C1)
             h2 = tmpp.tile([P, HC], F32, tag="h2", name="h2")
-            nc.scalar.activation(out=h2[:], in_=w[:], func=ACT.Square, bias=-C2, scale=C2)
-            nc.vector.scalar_tensor_tensor(out=a2[:], in0=w[:], scalar=2.0, in1=a2[:], op0=ALU.subtract, op1=ALU.mult)
-            nc.vector.scalar_tensor_tensor(out=h2[:], in0=w[:], scalar=1.0, in1=h2[:], op0=ALU.subtract, op1=ALU.mult)
-            nc.vector.tensor_scalar(out=a2[:], in0=a2[:], scalar1=0.0, scalar2=1.0 / 6.0, op0=ALU.min, op1=ALU.mult)
-            fb = tmpp.tile([P, HC], BF16, tag="fb", name="fb")
-            nc.vector.scalar_tensor_tensor(out=fb[:], in0=h2[:], scalar=0.0, in1=a2[:], op0=ALU.min, op1=ALU.subtract)
-            nc.vector.scalar_tensor_tensor(out=lo[:], in0=xv, scalar=mid / 11.0, in1=fb[:], op0=ALU.is_lt, op1=ALU.mult)
-            nc.vector.tensor_tensor(out=hi[:], in0=fb[:], in1=lo[:], op=ALU.subtract)
-            quantise_plane(rho, h, lo)
-            quantise_plane(rho + 4, h, hi)
+            nc.scalar.activation(out=h2[:], in_=tw[:], func=ACT.Square, bias=-C2, scale=C2)
+            nc.vector.tensor_tensor(out=a2[:], in0=a2[:], in1=tw[:], op=ALU.mult)
+            nc.vector.scalar_tensor_tensor(out=b2[:], in0=tw[:], scalar=2.0, in1=b2[:], op0=ALU.subtract, op1=ALU.mult)
+            nc.vector.scalar_tensor_tensor(out=h2[:], in0=tw[:], scalar=1.0, in1=h2[:], op0=ALU.subtract, op1=ALU.mult)
+            fa = tmpp.tile([P, HC], BF16, tag="fa", name="fa")
+            fc = tmpp.tile([P, HC], BF16, tag="fc", name="fc")
+            nc.vector.scalar_tensor_tensor(out=fa[:], in0=h2[:], scalar=0.0, in1=a2[:], op0=ALU.max, op1=ALU.subtract, reverse1=True)
+            nc.vector.scalar_tensor_tensor(out=fc[:], in0=h2[:], scalar=0.0, in1=b2[:], op0=ALU.min, op1=ALU.subtract)
+            n_a = new_plane(rho, h)
+            n_b = new_plane(rho + 4, h)
+            n_c = new_plane(rho + 2, h)
+            n_d = new_plane(rho + 6, h)
+            nc.vector.scalar_tensor_tensor(out=n_b[:], in0=y1[:], scalar=2.0, in1=fa[:], op0=ALU.is_lt, op1=ALU.mult)
+            if rho == 0:
+                nc.vector.scalar_tensor_tensor(out=n_a[:], in0=xv, scalar=4.0 / 11.0, in1=fa[:], op0=ALU.is_lt, op1=ALU.mult)
+            else:
+                nc.vector.scalar_tensor_tensor(out=fa[:], in0=xv, scalar=(rho + 4.0) / 11.0, in1=fa[:], op0=ALU.is_lt, op1=ALU.mult)
+                nc.vector.scalar_tensor_tensor(out=n_a[:], in0=xv, scalar=rho / 11.0, in1=fa[:], op0=ALU.is_ge, op1=ALU.mult)
+            nc.vector.scalar_tensor_tensor(out=fc[:], in0=y1[:], scalar=4.0, in1=fc[:], op0=ALU.is_lt, op1=ALU.mult)
+            nc.vector.scalar_tensor_tensor(out=n_c[:], in0=xv, scalar=cen / 11.0, in1=fc[:], op0=ALU.is_lt, op1=ALU.mult)
+            nc.vector.tensor_tensor(out=n_d[:], in0=fc[:], in1=n_c[:], op=ALU.subtract)
+            quantise_plane(rho + 4, h, n_b)
+            quantise_plane(rho, h, n_a)
+            quantise_plane(rho + 2, h, n_c)
+            quantise_plane(rho + 6, h, n_d)
 
         def low_unit_a(h):
             xv = xp[:, h, :, :, :].rearrange("p e b u -> p (e b u)")
             n8 = new_plane(8, h)
-            w = tmpp.tile([P, HC], F32, tag="w", name="w")
+            w = tmpp.tile([P, HC], F32, tag="tw", name="w")
             nc.scalar.activation(out=w[:], in_=xv, func=ACT.Abs, bias=-9.5, scale=11.0)
             a2 = tmpp.tile([P, HC], F32, tag="a2", name="a2")
             nc.vector.tensor_scalar(out=a2[:], in0=w[:], scalar1=1.5, scalar2=-1.5, op0=ALU.min, op1=ALU.add)
@@ -145,10 +168,10 @@ def tile_bsplinekan_kernel(tc, x, control_points, W_words, W_scales, b, gamma, b
             xv = xp[:, h, :, :, :].rearrange("p e b u -> p (e b u)")
             n9 = new_plane(9, h)
             n10 = new_plane(10, h)
-            w = tmpp.tile([P, HC], F32, tag="w", name="w")
+            w = tmpp.tile([P, HC], F32, tag="tw", name="w")
             nc.scalar.activation(out=w[:], in_=xv, func=ACT.Abs, bias=-10.0, scale=11.0)
             nc.scalar.activation(out=n9[:], in_=w[:], func=ACT.Relu, bias=1.0, scale=-1.0)
-            fb = tmpp.tile([P, HC], BF16, tag="fb", name="fb")
+            fb = tmpp.tile([P, HC], BF16, tag="fa", name="fb")
             nc.vector.tensor_scalar(out=fb[:], in0=xv, scalar1=1.0, scalar2=None, op0=ALU.is_lt)
             nc.vector.scalar_tensor_tensor(out=n10[:], in0=xv, scalar=10.0 / 11.0, in1=fb[:], op0=ALU.is_ge, op1=ALU.mult)
             quantise_plane(9, h, n9)
@@ -157,22 +180,19 @@ def tile_bsplinekan_kernel(tc, x, control_points, W_words, W_scales, b, gamma, b
         units = []
         for rho in range(2):
             for h in range(2):
-                units.append(("cubic", rho, h, (rho, rho + 4)))
+                units.append(("pair", rho, h, (rho + 4, rho, rho + 2, rho + 6)))
         for h in range(2):
             units.append(("low_a", 0, h, (8,)))
-        for h in range(2):
             units.append(("low_b", 0, h, (9, 10)))
-        for rho in range(2, 4):
-            for h in range(2):
-                units.append(("cubic", rho, h, (rho, rho + 4)))
         n_woven = len(units) - TRAIL
         n_banks = NCHUNK * NK
 
         plan = []
+        pend = []
         for g in range(2):
             for h in range(2):
                 for q in range(2):
-                    plan.append(("lin", g, h, q))
+                    pend.append(("lin", g, h, q))
         ready = []
         halves_done = 0
 
@@ -180,7 +200,7 @@ def tile_bsplinekan_kernel(tc, x, control_points, W_words, W_scales, b, gamma, b
             plan.append(("unit", unit))
             for k in unit[3]:
                 for q in range(halves_done):
-                    plan.append(("mx", k, unit[2], q))
+                    pend.append(("mx", k, unit[2], q))
                 ready.append((k, unit[2]))
 
         plan_unit(units[0])
@@ -190,14 +210,21 @@ def tile_bsplinekan_kernel(tc, x, control_points, W_words, W_scales, b, gamma, b
             plan.append(("bank", c, wd, bank))
             if wd == NK - 1 and c % 4 == 3:
                 for (k, h) in ready:
-                    plan.append(("mx", k, h, halves_done))
+                    pend.append(("mx", k, h, halves_done))
                 halves_done += 1
             if n_given < n_woven and (bank + 1) * (n_woven - 1) >= n_given * n_banks:
                 plan_unit(units[n_given])
                 n_given += 1
+            if bank % MX_EVERY == MX_EVERY - 1 and bank >= 8:
+                for rep in range(MX_RUN):
+                    if pend:
+                        plan.append(pend.pop(0))
         while n_given < len(units):
+            plan.extend(pend)
+            pend = []
             plan_unit(units[n_given])
             n_given += 1
+        plan.extend(pend)
         last = {}
         for n, act in enumerate(plan):
             if act[0] == "mx":
@@ -222,8 +249,8 @@ def tile_bsplinekan_kernel(tc, x, control_points, W_words, W_scales, b, gamma, b
                 )
             elif act[0] == "unit":
                 kind, rho, h = act[1][0], act[1][1], act[1][2]
-                if kind == "cubic":
-                    cubic_unit(rho, h)
+                if kind == "pair":
+                    pair_unit(rho, h)
                 elif kind == "low_a":
                     low_unit_a(h)
                 else:

from contextlib import ExitStack

from concourse import mybir
from concourse.masks import make_identity

F32 = mybir.dt.float32
BF16 = mybir.dt.bfloat16
U8 = mybir.dt.uint8
U32 = mybir.dt.uint32
I32 = mybir.dt.int32
FP8X4 = mybir.dt.float8_e4m3fn_x4
FP4X4 = mybir.dt.float4_e2m1fn_x4
ALU = mybir.AluOpType
ACT = mybir.ActivationFunctionType

P = 128
B = 256
IN_F = 1024
OUT_F = 1024
NK = 11
EPS = 1e-5
FLOPS = 2 * B * OUT_F * (IN_F * NK + IN_F)

NCHUNK = OUT_F // P
NSLOT = 2 * NK
WORDS_Q = 128 * NK
HC = 1024
TRAIL = 4
MX_EVERY = 2
MX_RUN = 2


def tile_bsplinekan_kernel(tc, x, control_points, W_words, W_scales, b, gamma, beta, out):
    nc = tc.nc
    with ExitStack() as ctx:
        const = ctx.enter_context(tc.tile_pool(name="const", bufs=1))
        rawp = ctx.enter_context(tc.tile_pool(name="rawp", bufs=2))
        grpp = ctx.enter_context(tc.tile_pool(name="grpp", bufs=4))
        tmpp = ctx.enter_context(tc.tile_pool(name="tmpp", bufs=1))
        lnp = ctx.enter_context(tc.tile_pool(name="lnp", bufs=2))
        pacc = ctx.enter_context(tc.psum_pool(name="pacc", bufs=1))
        ptr = ctx.enter_context(tc.psum_pool(name="ptr", bufs=4))

        with tc.tile_pool(name="xin", bufs=1) as xin:
            x_sb = xin.tile([P, 2, IN_F], BF16)
            nc.sync.dma_start(out=x_sb[:], in_=x.rearrange("(h p) i -> p h i", p=P))

            cpv = control_points.rearrange("(c p) i k -> c p (i k)", p=P)
            raws = []
            for c in range(2):
                raw = rawp.tile([P, IN_F * NK], BF16, tag="raw", name="raw%d" % c)
                nc.sync.dma_start(out=raw[:], in_=cpv[c])
                raws.append(raw)

            ws = const.tile([P, 2, OUT_F], U8, align_bytes=64)
            nc.vector.memset(ws[:].bitcast(I32), 0)
            wt = const.tile([P, 2, 2 * OUT_F], U8, align_bytes=64)
            nc.sync.dma_start(out=wt[:].bitcast(I32), in_=W_words.bitcast(I32).rearrange("g p n -> p g n"))
            wsv = W_scales.bitcast(I32)
            for r in range(4):
                nc.sync.dma_start(
                    out=ws[r:P:32, :, :].bitcast(I32),
                    in_=wsv[:, r:16:4, :].rearrange("g q n -> q g n"),
                )

            ident = const.tile([P, P], F32)
            make_identity(nc, ident[:])

            xp = const.tile([P, 2, 2, P, 4], BF16)
            xg = xin.tile([P, 2, B, 4], BF16, align_bytes=64)
            for h in range(2):
                xw = x_sb[:, h, :].bitcast(F32)
                pxs = ptr.tile([P, 4, P], F32, tag="pt", name="pxs%d" % h)
                for u in range(4):
                    nc.tensor.transpose(pxs[:, u, :], xw[:, P * u:P * (u + 1)], ident[:])
                src = pxs[:].bitcast(BF16).rearrange("p u (b e) -> p e b u", e=2)
                if h == 0:
                    nc.scalar.copy(out=xp[:, h, :, :, :], in_=src)
                else:
                    nc.vector.tensor_copy(out=xp[:, h, :, :, :], in_=src)
            for h in range(2):
                xw = x_sb[:, h, :].bitcast(F32)
                pxl = ptr.tile([P, 4, P], F32, tag="pt", name="pxl%d" % h)
                for g in range(2):
                    for u in range(2):
                        nc.tensor.transpose(pxl[:, 2 * g + u, :], xw[:, 256 * g + u:256 * (g + 1):2], ident[:])
                nc.vector.tensor_copy(
                    out=xg[:, :, h * P:(h + 1) * P, :].bitcast(F32),
                    in_=pxl[:].rearrange("p (g u) b -> p g b u", u=2),
                )
            xcodes = const.tile([P, 2 * B], U32, align_bytes=64)
            xscales = const.tile([P, 2 * B], U8, align_bytes=64)
            nc.vector.quantize_mx(
                out=xcodes[:].bitcast(FP8X4),
                scales=xscales[:],
                in_=xg[:].rearrange("p g b t -> p (g b t)"),
            )

        nbp = ctx.enter_context(tc.tile_pool(name="nbp", bufs=5))

        bcodes = const.tile([P, NK, 2, 2 * P], U32, align_bytes=64)
        bscales = const.tile([P, NK, 2, 2 * P], U8, align_bytes=64)

        def new_plane(k, h):
            return nbp.tile([P, HC], BF16, tag="nb", name="nb%d_%d" % (k, h), align_bytes=64)

        def quantise_plane(k, h, nb):
            nc.vector.quantize_mx(out=bcodes[:, k, h, :].bitcast(FP8X4), scales=bscales[:, k, h, :], in_=nb[:])

        C2 = (2.0 / 3.0) ** 0.5

        C1 = (1.0 / 6.0) ** 0.5

        def pair_unit(rho, h):
            xv = xp[:, h, :, :, :].rearrange("p e b u -> p (e b u)")
            cen = float(rho + 6)
            y1 = tmpp.tile([P, HC], F32, tag="y1", name="y1")
            nc.scalar.activation(out=y1[:], in_=xv, func=ACT.Abs, bias=-cen, scale=11.0)
            tw = tmpp.tile([P, HC], F32, tag="tw", name="tw")
            nc.scalar.activation(out=tw[:], in_=y1[:], func=ACT.Abs, bias=-4.0)
            nc.scalar.activation(out=tw[:], in_=tw[:], func=ACT.Abs, bias=-2.0)
            a2 = tmpp.tile([P, HC], F32, tag="a2", name="a2")
            nc.scalar.activation(out=a2[:], in_=tw[:], func=ACT.Square, scale=C1)
            b2 = tmpp.tile([P, HC], F32, tag="b2", name="b2")
            nc.scalar.activation(out=b2[:], in_=tw[:], func=ACT.Square, bias=-2.0 * C1, scale=C1)
            h2 = tmpp.tile([P, HC], F32, tag="h2", name="h2")
            nc.scalar.activation(out=h2[:], in_=tw[:], func=ACT.Square, bias=-C2, scale=C2)
            nc.vector.tensor_tensor(out=a2[:], in0=a2[:], in1=tw[:], op=ALU.mult)
            nc.vector.scalar_tensor_tensor(out=b2[:], in0=tw[:], scalar=2.0, in1=b2[:], op0=ALU.subtract, op1=ALU.mult)
            nc.vector.scalar_tensor_tensor(out=h2[:], in0=tw[:], scalar=1.0, in1=h2[:], op0=ALU.subtract, op1=ALU.mult)
            fa = tmpp.tile([P, HC], BF16, tag="fa", name="fa")
            fc = tmpp.tile([P, HC], BF16, tag="fc", name="fc")
            nc.vector.scalar_tensor_tensor(out=fa[:], in0=h2[:], scalar=0.0, in1=a2[:], op0=ALU.max, op1=ALU.subtract, reverse1=True)
            nc.vector.scalar_tensor_tensor(out=fc[:], in0=h2[:], scalar=0.0, in1=b2[:], op0=ALU.min, op1=ALU.subtract)
            n_a = new_plane(rho, h)
            n_b = new_plane(rho + 4, h)
            n_c = new_plane(rho + 2, h)
            n_d = new_plane(rho + 6, h)
            nc.vector.scalar_tensor_tensor(out=n_b[:], in0=y1[:], scalar=2.0, in1=fa[:], op0=ALU.is_lt, op1=ALU.mult)
            if rho == 0:
                nc.vector.scalar_tensor_tensor(out=n_a[:], in0=xv, scalar=4.0 / 11.0, in1=fa[:], op0=ALU.is_lt, op1=ALU.mult)
            else:
                nc.vector.scalar_tensor_tensor(out=fa[:], in0=xv, scalar=(rho + 4.0) / 11.0, in1=fa[:], op0=ALU.is_lt, op1=ALU.mult)
                nc.vector.scalar_tensor_tensor(out=n_a[:], in0=xv, scalar=rho / 11.0, in1=fa[:], op0=ALU.is_ge, op1=ALU.mult)
            nc.vector.scalar_tensor_tensor(out=fc[:], in0=y1[:], scalar=4.0, in1=fc[:], op0=ALU.is_lt, op1=ALU.mult)
            nc.vector.scalar_tensor_tensor(out=n_c[:], in0=xv, scalar=cen / 11.0, in1=fc[:], op0=ALU.is_lt, op1=ALU.mult)
            nc.vector.tensor_tensor(out=n_d[:], in0=fc[:], in1=n_c[:], op=ALU.subtract)
            quantise_plane(rho + 4, h, n_b)
            quantise_plane(rho, h, n_a)
            quantise_plane(rho + 2, h, n_c)
            quantise_plane(rho + 6, h, n_d)

        def low_unit_a(h):
            xv = xp[:, h, :, :, :].rearrange("p e b u -> p (e b u)")
            n8 = new_plane(8, h)
            w = tmpp.tile([P, HC], F32, tag="tw", name="w")
            nc.scalar.activation(out=w[:], in_=xv, func=ACT.Abs, bias=-9.5, scale=11.0)
            a2 = tmpp.tile([P, HC], F32, tag="a2", name="a2")
            nc.vector.tensor_scalar(out=a2[:], in0=w[:], scalar1=1.5, scalar2=-1.5, op0=ALU.min, op1=ALU.add)
            nc.scalar.activation(out=a2[:], in_=a2[:], func=ACT.Square, scale=0.5 ** 0.5)
            h2 = tmpp.tile([P, HC], F32, tag="h2", name="h2")
            nc.vector.tensor_scalar(out=h2[:], in0=w[:], scalar1=0.5, scalar2=-0.5, op0=ALU.min, op1=ALU.add)
            nc.scalar.activation(out=h2[:], in_=h2[:], func=ACT.Square, scale=1.5 ** 0.5)
            nc.vector.tensor_tensor(out=n8[:], in0=a2[:], in1=h2[:], op=ALU.subtract)
            quantise_plane(8, h, n8)

        def low_unit_b(h):
            xv = xp[:, h, :, :, :].rearrange("p e b u -> p (e b u)")
            n9 = new_plane(9, h)
            n10 = new_plane(10, h)
            w = tmpp.tile([P, HC], F32, tag="tw", name="w")
            nc.scalar.activation(out=w[:], in_=xv, func=ACT.Abs, bias=-10.0, scale=11.0)
            nc.scalar.activation(out=n9[:], in_=w[:], func=ACT.Relu, bias=1.0, scale=-1.0)
            fb = tmpp.tile([P, HC], BF16, tag="fa", name="fb")
            nc.vector.tensor_scalar(out=fb[:], in0=xv, scalar1=1.0, scalar2=None, op0=ALU.is_lt)
            nc.vector.scalar_tensor_tensor(out=n10[:], in0=xv, scalar=10.0 / 11.0, in1=fb[:], op0=ALU.is_ge, op1=ALU.mult)
            quantise_plane(9, h, n9)
            quantise_plane(10, h, n10)

        units = []
        for rho in range(2):
            for h in range(2):
                units.append(("pair", rho, h, (rho + 4, rho, rho + 2, rho + 6)))
        for h in range(2):
            units.append(("low_a", 0, h, (8,)))
            units.append(("low_b", 0, h, (9, 10)))
        n_woven = len(units) - TRAIL
        n_banks = NCHUNK * NK

        plan = []
        pend = []
        for g in range(2):
            for h in range(2):
                for q in range(2):
                    pend.append(("lin", g, h, q))
        ready = []
        halves_done = 0

        def plan_unit(unit):
            plan.append(("unit", unit))
            for k in unit[3]:
                for q in range(halves_done):
                    pend.append(("mx", k, unit[2], q))
                ready.append((k, unit[2]))

        plan_unit(units[0])
        n_given = 1
        for bank in range(n_banks):
            c, wd = divmod(bank, NK)
            plan.append(("bank", c, wd, bank))
            if wd == NK - 1 and c % 4 == 3:
                for (k, h) in ready:
                    pend.append(("mx", k, h, halves_done))
                halves_done += 1
            if n_given < n_woven and (bank + 1) * (n_woven - 1) >= n_given * n_banks:
                plan_unit(units[n_given])
                n_given += 1
            if bank % MX_EVERY == MX_EVERY - 1 and bank >= 8:
                for rep in range(MX_RUN):
                    if pend:
                        plan.append(pend.pop(0))
        while n_given < len(units):
            plan.extend(pend)
            pend = []
            plan_unit(units[n_given])
            n_given += 1
        plan.extend(pend)
        last = {}
        for n, act in enumerate(plan):
            if act[0] == "mx":
                last[(act[2], act[3])] = n

        ccodes = const.tile([P, 2, NSLOT, 512], U32, align_bytes=64)
        cscales = const.tile([P, 2, NSLOT, 512], U8, align_bytes=64)
        acc = [[pacc.tile([P, 512], F32, tag="acc%d%d" % (h, q), name="acc%d%d" % (h, q)) for q in range(2)] for h in range(2)]
        raw_of = {}
        for n, act in enumerate(plan):
            if act[0] == "lin":
                g, h, q = act[1], act[2], act[3]
                col = g * B + h * P
                nc.tensor.matmul_mx(
                    out=acc[h][q][:],
                    lhsT=xcodes[:, col:col + P].bitcast(FP8X4),
                    lhsT_scale=xscales[:, col:col + P],
                    rhs=wt[:, g, 1024 * q:1024 * (q + 1)].bitcast(FP4X4),
                    rhs_scale=ws[:, g, 512 * q:512 * (q + 1)],
                    start=(g == 0),
                    stop=False,
                )
            elif act[0] == "unit":
                kind, rho, h = act[1][0], act[1][1], act[1][2]
                if kind == "pair":
                    pair_unit(rho, h)
                elif kind == "low_a":
                    low_unit_a(h)
                else:
                    low_unit_b(h)
            elif act[0] == "mx":
                k, h, q = act[1], act[2], act[3]
                for par in range(2):
                    f = par * NK + k
                    nc.tensor.matmul_mx(
                        out=acc[h][q][:],
                        lhsT=bcodes[:, k, h, par * P:(par + 1) * P].bitcast(FP8X4),
                        lhsT_scale=bscales[:, k, h, par * P:(par + 1) * P],
                        rhs=ccodes[:, q, f, :].bitcast(FP8X4),
                        rhs_scale=cscales[:, q, f, :],
                        start=False,
                        stop=(par == 1 and last[(h, q)] == n),
                    )
            else:
                c, wd, bank = act[1], act[2], act[3]
                if wd == 0:
                    if c < 2:
                        raw_of[c] = raws[c]
                    else:
                        raw = rawp.tile([P, IN_F * NK], BF16, tag="raw", name="raw%d" % c)
                        nc.sync.dma_start(out=raw[:], in_=cpv[c])
                        raw_of[c] = raw
                raww = raw_of[c][:].bitcast(F32)
                pt = ptr.tile([P, 4, P], F32, tag="pt", name="pt")
                for u in range(4):
                    st = WORDS_Q * u + wd
                    nc.tensor.transpose(pt[:, u, :], raww[:, st:st + NK * 127 + 1:NK], ident[:])
                grp = grpp.tile([P, 2, P, 4], BF16, tag="grp", name="grp", align_bytes=64)
                src = pt[:].bitcast(BF16).rearrange("p u (o e) -> p e o u", e=2)
                nc.any.tensor_copy(out=grp[:], in_=src)
                q, c4 = divmod(c, 4)
                for e in range(2):
                    f = 2 * wd + e
                    nc.vector.quantize_mx(
                        out=ccodes[:, q, f, c4 * P:(c4 + 1) * P].bitcast(FP8X4),
                        scales=cscales[:, q, f, c4 * P:(c4 + 1) * P],
                        in_=grp[:, e, :, :].rearrange("p o u -> p (o u)"),
                    )

        gb = rawp.tile([P, 3, OUT_F], BF16, tag="raw", name="gb")
        nc.sync.dma_start(out=gb[:, 0, :], in_=b.partition_broadcast(P))
        nc.sync.dma_start(out=gb[:, 1, :], in_=gamma.partition_broadcast(P))
        nc.sync.dma_start(out=gb[:, 2, :], in_=beta.partition_broadcast(P))
        yt = rawp.tile([P, 2, OUT_F], F32, tag="raw", name="yt")
        for h in range(2):
            y = yt[:, h, :]
            stats = lnp.tile([P, 2, 6], F32, tag="stats", name="stats")
            for q in range(2):
                sl = slice(q * 512, (q + 1) * 512)
                nc.vector.tensor_tensor(out=yt[:, h, sl], in0=acc[h][q][:], in1=gb[:, 0, sl], op=ALU.add)
                nc.vector.bn_stats(out=stats[:, q, :], in_=yt[:, h, sl])
            mv = lnp.tile([P, 2], F32, tag="mv", name="mv")
            nc.vector.bn_aggr(out=mv[:], in_=stats[:].rearrange("p q s -> p (q s)"))
            rstd = lnp.tile([P, 1], F32, tag="rstd", name="rstd")
            nc.scalar.activation(out=rstd[:], in_=mv[:, 1:2], func=ACT.Sqrt, bias=EPS)
            nc.vector.reciprocal(out=rstd[:], in_=rstd[:])
            nc.vector.scalar_tensor_tensor(out=y, in0=y, scalar=mv[:, 0:1], in1=gb[:, 1, :], op0=ALU.subtract, op1=ALU.mult)
            nc.vector.scalar_tensor_tensor(out=y, in0=y, scalar=rstd[:], in1=gb[:, 2, :], op0=ALU.mult, op1=ALU.add)
            nc.sync.dma_start(out=out[h * P:(h + 1) * P, :], in_=y)
